import numpy as np
import ml_dtypes


def mxq(x, axis, fmt="e4m3"):
    dtype, down = {"e4m3": (ml_dtypes.float8_e4m3fn, 7), "e5m2": (ml_dtypes.float8_e5m2, 14)}[fmt]
    v = np.moveaxis(np.asarray(x, np.float32).astype(ml_dtypes.bfloat16).astype(np.float64), axis, -1)
    blocks = v.reshape(v.shape[:-1] + (-1, 32))
    amax = np.abs(blocks).max(-1, keepdims=True)
    byte = np.maximum(np.where(amax > 0, np.frexp(amax)[1] - 1 + 127, 0) - down, 1)
    scale = np.exp2(byte - 127.0)
    codes = (blocks / scale).astype(np.float32).astype(dtype).astype(np.float64)
    return np.moveaxis((codes * scale).reshape(v.shape), -1, axis)


WIDE = False


def mx_kscale(k):
    if not WIDE:
        return np.ones(k)
    levels = np.array([10, -10, 5, -5, 0])
    a = np.random.permutation(np.resize(levels, k // 512 * 4)).reshape(k // 512, 4)
    idx = np.arange(k)
    return np.exp2(a[idx // 512, idx % 128 // 32])


BF16 = ml_dtypes.bfloat16


def bf(x):
    return np.asarray(x, np.float32).astype(BF16)


def f64(x):
    return np.asarray(x).astype(np.float64)


NS, NT, DS, DT, DH, DB, DO, NF, SP = 512, 1024, 1024, 128, 1024, 1024, 512, 2, 16
EPS_ROW = 1e-8
EPS_BN = 1e-5


def row_norm(a):
    return a / np.maximum(a.sum(axis=1, keepdims=True), EPS_ROW)


def bn_eval(x, gamma, beta, mean, var):
    return (x - mean) * (gamma / np.sqrt(var + EPS_BN)) + beta


def setup_inputs():
    t = mx_kscale(DH)
    edges = np.random.random((NT, NS)) < 1.0 / SP
    linked = np.random.random((1, NS)) > 0.03
    return {"h_tgt": bf(np.maximum(np.random.standard_normal((NT, DH)) * 1.25, 0.0) * t),
            "A": bf(np.random.random((NT, NS)) * edges * linked),
            "Wb0": bf(np.random.standard_normal((DH, DB)) * 4.0 / np.sqrt(DH) / t[:, None]),
            "bb0": bf(np.random.standard_normal(DB) * 0.1),
            "bn_b_gamma": bf(np.random.uniform(0.5, 1.5, DB)),
            "bn_b_beta": bf(np.random.standard_normal(DB) * 0.1),
            "bn_b_mean": bf(np.random.standard_normal(DB) * 0.1),
            "bn_b_var": bf(np.random.uniform(0.5, 1.5, DB))}


def reference(h_tgt, A, Wb0, bb0, bn_b_gamma, bn_b_beta, bn_b_mean, bn_b_var):
    at_n = row_norm(f64(A).T)
    agg = mxq(at_n, 1, "e4m3") @ mxq(f64(h_tgt), 0, "e4m3")
    h = (mxq(agg, 1, "e4m3") @ mxq(f64(Wb0), 0, "e4m3")) + f64(bb0)
    return np.maximum(bn_eval(h, f64(bn_b_gamma), f64(bn_b_beta), f64(bn_b_mean), f64(bn_b_var)), 0.0)

@@ -1,0 +1,297 @@
+from contextlib import ExitStack
+
+import concourse.mybir as mybir
+from concourse.masks import make_identity
+
+FP8X4 = mybir.dt.float8_e4m3fn_x4
+BF16 = mybir.dt.bfloat16
+F32 = mybir.dt.float32
+U32 = mybir.dt.uint32
+U8 = mybir.dt.uint8
+ALU = mybir.AluOpType
+ACT = mybir.ActivationFunctionType
+AX = mybir.AxisListType
+
+P = 128
+PACK = 4
+K_PASS = P * PACK
+NS, NT, DH, DB = 512, 1024, 1024, 1024
+HALF = 256
+EPS_ROW = 1e-8
+EPS_BN = 1e-5
+FLOPS = 2 * NS * NT * DH + 2 * NS * DH * DB
+
+
+def tile_bipartitegcnstack_pb_kernel(
+    tc, h_tgt, A, Wb0, bb0, bn_b_gamma, bn_b_beta, bn_b_mean, bn_b_var, out
+):
+    nc = tc.nc
+    with ExitStack() as ctx:
+        keep = ctx.enter_context(tc.tile_pool(name="keep", bufs=1))
+        psum = ctx.enter_context(tc.psum_pool(name="psum", bufs=8))
+        ctx.enter_context(tc.manual_schedule())
+
+        copies = {"v": nc.vector.tensor_copy, "s": nc.scalar.copy}
+
+        a_raw = [keep.tile([P, PACK, NS], BF16, name="a_raw%d" % c) for c in range(2)]
+        h_raw = [keep.tile([P, PACK, DH], BF16, name="h_raw%d" % c) for c in range(2)]
+        w_raw = [keep.tile([P, 2 * PACK, 512], BF16, name="w_raw%d" % f) for f in range(2)]
+        a_grp = [keep.tile([P, 2, HALF, PACK], BF16, name="a_grp%d" % hh, align_bytes=64) for hh in range(2)]
+        g_grp = [keep.tile([P, NS, PACK], BF16, name="g_grp%d" % g, align_bytes=64) for g in range(2)]
+        h_grp = {}
+        w_grp = {}
+        for x in range(2):
+            for y in range(2):
+                h_grp[(x, y)] = keep.tile([P, 512, PACK], BF16, name="h_grp%d%d" % (x, y), align_bytes=64)
+                w_grp[(x, y)] = keep.tile([P, 512, PACK], BF16, name="w_grp%d%d" % (x, y), align_bytes=64)
+        a_codes = [keep.tile([P, 2 * HALF], U32, name="a_codes%d" % hh, align_bytes=64) for hh in range(2)]
+        a_scales = [keep.tile([P, 2 * HALF], U8, name="a_scales%d" % hh, align_bytes=64) for hh in range(2)]
+        h_codes = keep.tile([P, 2, DH], U32, name="h_codes", align_bytes=64)
+        h_scales = keep.tile([P, 2, DH], U8, name="h_scales", align_bytes=64)
+        w_codes = keep.tile([P, 2, DB], U32, name="w_codes", align_bytes=64)
+        w_scales = keep.tile([P, 2, DB], U8, name="w_scales", align_bytes=64)
+        g_codes = keep.tile([P, 2, NS], U32, name="g_codes", align_bytes=64)
+        g_scales = keep.tile([P, 2, NS], U8, name="g_scales", align_bytes=64)
+        y_t = [keep.tile([P, NS], F32, name="y_t%d" % j) for j in range(8)]
+
+        vec_rows = keep.tile([P, P], BF16, name="vec_rows")
+        nc.vector.memset(vec_rows[:], 0.0)
+        for v, vec in enumerate((bb0, bn_b_gamma, bn_b_beta, bn_b_mean, bn_b_var)):
+            nc.scalar.dma_start(
+                out=vec_rows[8 * v : 8 * v + 8, :], in_=vec.rearrange("(r c) -> r c", c=P)
+            )
+        for c in range(2):
+            nc.sync.dma_start(
+                out=a_raw[c][:],
+                in_=A[K_PASS * c : K_PASS * (c + 1), :].rearrange("(p j) s -> p j s", j=PACK),
+            )
+        for c in range(2):
+            nc.sync.dma_start(
+                out=h_raw[c][:],
+                in_=h_tgt[K_PASS * c : K_PASS * (c + 1), :].rearrange("(p j) d -> p j d", j=PACK),
+            )
+        for f in range(2):
+            nc.sync.dma_start(
+                out=w_raw[f][:], in_=Wb0[:, 512 * f : 512 * (f + 1)].rearrange("(r p) o -> p r o", p=P)
+            )
+        warm_in = keep.tile([P, 1], F32, name="warm_in")
+        nc.vector.memset(warm_in[:], 1.0)
+        warm_out = keep.tile([P, 1], F32, name="warm_out")
+        nc.scalar.sqrt(out=warm_out[:], in_=warm_in[:])
+        ident_f = keep.tile([P, P], F32, name="ident_f")
+        make_identity(nc, ident_f[:])
+        ones = keep.tile([P, 64], BF16, name="ones")
+        nc.vector.memset(ones[:], 1.0)
+        ident_b = keep.tile([P, P], BF16, name="ident_b")
+        nc.vector.tensor_copy(out=ident_b[:], in_=ident_f[:])
+
+        vec_ps = psum.tile([P, P], BF16, tag="bank", name="vec_ps")
+        nc.tensor.transpose(vec_ps[:], vec_rows[:], ident_b[:])
+        vec_t = keep.tile([P, 40], F32, name="vec_t")
+        nc.vector.tensor_copy(out=vec_t[:], in_=vec_ps[:, 0:40])
+        var_eps = keep.tile([P, 8], F32, name="var_eps")
+        nc.vector.tensor_scalar_add(out=var_eps[:], in0=vec_t[:, 32:40], scalar1=EPS_BN)
+        std = keep.tile([P, 8], F32, name="std")
+        nc.scalar.sqrt(out=std[:], in_=var_eps[:])
+        rstd = keep.tile([P, 8], F32, name="rstd")
+        nc.vector.reciprocal(out=rstd[:], in_=std[:])
+        sc = keep.tile([P, 8], F32, name="sc")
+        nc.vector.tensor_tensor(out=sc[:], in0=vec_t[:, 8:16], in1=rstd[:], op=ALU.mult)
+        diff = keep.tile([P, 8], F32, name="diff")
+        nc.vector.tensor_tensor(out=diff[:], in0=vec_t[:, 0:8], in1=vec_t[:, 24:32], op=ALU.subtract)
+        prod = keep.tile([P, 8], F32, name="prod")
+        nc.vector.tensor_tensor(out=prod[:], in0=diff[:], in1=sc[:], op=ALU.mult)
+        sh = keep.tile([P, 8], F32, name="sh")
+        nc.vector.tensor_tensor(out=sh[:], in0=prod[:], in1=vec_t[:, 16:24], op=ALU.add)
+
+        cs_ps = psum.tile([P, 2, 4, 64], F32, tag="bank", name="cs_ps")
+        for c in range(2):
+            for i in range(4):
+                for j in range(PACK):
+                    nc.tensor.matmul(
+                        out=cs_ps[:, c, i, :],
+                        lhsT=a_raw[c][:, j, P * i : P * (i + 1)],
+                        rhs=ones[:],
+                        start=(j == 0),
+                        stop=(j == PACK - 1),
+                    )
+        cs = keep.tile([P, 4], F32, name="cs")
+        nc.vector.tensor_reduce(
+            out=cs[:], in_=cs_ps[:, :, :, 0].rearrange("p c i -> p i c"), axis=AX.X, op=ALU.add
+        )
+        cs_cl = keep.tile([P, 4], F32, name="cs_cl")
+        nc.vector.tensor_scalar_max(out=cs_cl[:], in0=cs[:], scalar1=EPS_ROW)
+        rec = keep.tile([P, 4], F32, name="rec")
+        nc.vector.reciprocal(out=rec[:], in_=cs_cl[:])
+        rec_rep = keep.tile([P, 4, P], F32, name="rec_rep")
+        nc.vector.tensor_copy(out=rec_rep[:], in_=rec[:].unsqueeze(2).to_broadcast([P, 4, P]))
+        r_bc = psum.tile([P, NS], F32, tag="bank", name="r_bc")
+        for i in range(4):
+            nc.tensor.transpose(r_bc[:, P * i : P * (i + 1)], rec_rep[:, i, :], ident_f[:])
+
+        def regroup(eng, dst, src):
+            copies[eng](
+                out=dst.rearrange("p (q i) j -> p q j i", i=4),
+                in_=src.rearrange("p j (q i) -> p q j i", i=4),
+            )
+
+        def quantise(codes, scales, grouped):
+            nc.vector.quantize_mx(out=codes.bitcast(FP8X4), scales=scales, in_=grouped)
+
+        def regroup_h(c, g, eng):
+            regroup(eng, h_grp[(c, g)][:], h_raw[c][:, :, 512 * g : 512 * (g + 1)])
+
+        def quantise_h(c, g):
+            cols = slice(512 * g, 512 * (g + 1))
+            quantise(h_codes[:, c, cols], h_scales[:, c, cols], h_grp[(c, g)][:].rearrange("p w j -> p (w j)"))
+
+        def regroup_w(g, f, eng):
+            regroup(eng, w_grp[(g, f)][:], w_raw[f][:, PACK * g : PACK * (g + 1), :])
+
+        def quantise_w(g, f):
+            cols = slice(512 * f, 512 * (f + 1))
+            quantise(w_codes[:, g, cols], w_scales[:, g, cols], w_grp[(g, f)][:].rearrange("p w j -> p (w j)"))
+
+        def normalise_a(c, hh):
+            cols = slice(HALF * hh, HALF * (hh + 1))
+            nc.vector.tensor_tensor(
+                out=a_grp[hh][:, c].rearrange("p (q i) j -> p q j i", i=4),
+                in0=a_raw[c][:, :, cols].rearrange("p j (q i) -> p q j i", i=4),
+                in1=r_bc[:, cols].rearrange("p (q i) -> p q i", i=4).unsqueeze(2).to_broadcast([P, HALF // 4, PACK, 4]),
+                op=ALU.mult,
+            )
+
+        def quantise_a(hh):
+            quantise(a_codes[hh][:], a_scales[hh][:], a_grp[hh][:].rearrange("p c s j -> p (c s j)"))
+
+        agg_ps = {}
+
+        def agg_block(hh, g, b):
+            bank = psum.tile([P, PACK, P], F32, tag="bank", name="agg_ps")
+            agg_ps[(hh, g, b)] = bank
+            for t in range(PACK):
+                d_cols = slice(K_PASS * g + P * t, K_PASS * g + P * (t + 1))
+                for c in range(2):
+                    s_cols = slice(HALF * c + P * b, HALF * c + P * (b + 1))
+                    nc.tensor.matmul_mx(
+                        out=bank[:, t, :],
+                        lhsT=h_codes[:, c, d_cols].bitcast(FP8X4),
+                        lhsT_scale=h_scales[:, c, d_cols],
+                        rhs=a_codes[hh][:, s_cols].bitcast(FP8X4),
+                        rhs_scale=a_scales[hh][:, s_cols],
+                        start=(c == 0),
+                        stop=(c == 1),
+                    )
+
+        def agg_out(hh, g, b, eng):
+            s0 = HALF * hh + P * b
+            copies[eng](out=g_grp[g][:, s0 : s0 + P, :], in_=agg_ps[(hh, g, b)][:].rearrange("p t s -> p s t"))
+
+        def quantise_agg(hh, g):
+            cols = slice(HALF * hh, HALF * (hh + 1))
+            quantise(g_codes[:, g, cols], g_scales[:, g, cols], g_grp[g][:, cols, :].rearrange("p s t -> p (s t)"))
+
+        h_ps = {}
+
+        def layer_pass(j, g):
+            if g == 0:
+                h_ps[j] = psum.tile([P, NS], F32, tag="bank", name="h_ps")
+            o_cols = slice(P * j, P * (j + 1))
+            nc.tensor.matmul_mx(
+                out=h_ps[j][:],
+                lhsT=w_codes[:, g, o_cols].bitcast(FP8X4),
+                lhsT_scale=w_scales[:, g, o_cols],
+                rhs=g_codes[:, g, :].bitcast(FP8X4),
+                rhs_scale=g_scales[:, g, :],
+                start=(g == 0),
+                stop=(g == 1),
+            )
+
+        def scale_shift(j, eng):
+            if eng == "s":
+                nc.scalar.activation(
+                    out=y_t[j][:], in_=h_ps[j][:], func=ACT.Identity, bias=sh[:, j : j + 1], scale=sc[:, j : j + 1]
+                )
+            else:
+                nc.vector.tensor_scalar(
+                    out=y_t[j][:], in0=h_ps[j][:], scalar1=sc[:, j : j + 1], scalar2=sh[:, j : j + 1],
+                    op0=ALU.mult, op1=ALU.add,
+                )
+
+        o_ps = {}
+
+        def turn_back(i, f):
+            bank = psum.tile([P, 512], F32, tag="bank", name="o_ps")
+            o_ps[(i, f)] = bank
+            for jj in range(4):
+                nc.tensor.transpose(
+                    bank[:, P * jj : P * (jj + 1)], y_t[4 * f + jj][:, P * i : P * (i + 1)], ident_f[:]
+                )
+
+        def relu_store(i, f, eng):
+            o_sb = keep.tile([P, 512], F32, name="o_sb%d%d" % (i, f))
+            if eng == "s":
+                nc.scalar.activation(out=o_sb[:], in_=o_ps[(i, f)][:], func=ACT.Relu)
+            else:
+                nc.vector.tensor_scalar_max(out=o_sb[:], in0=o_ps[(i, f)][:], scalar1=0.0)
+            nc.sync.dma_start(out=out[P * i : P * (i + 1), 512 * f : 512 * (f + 1)], in_=o_sb[:])
+
+        regroup_h(0, 0, "v")
+        regroup_h(0, 1, "s")
+        normalise_a(0, 0)
+        normalise_a(1, 0)
+        regroup_h(1, 0, "s")
+        regroup_h(1, 1, "s")
+        quantise_h(0, 0)
+        quantise_a(0)
+        quantise_h(1, 0)
+        agg_block(0, 0, 0)
+        agg_block(0, 0, 1)
+        quantise_h(0, 1)
+        quantise_h(1, 1)
+        agg_block(0, 1, 0)
+        agg_block(0, 1, 1)
+        normalise_a(0, 1)
+        normalise_a(1, 1)
+        quantise_a(1)
+        for g in range(2):
+            for b in range(2):
+                agg_block(1, g, b)
+        regroup_w(0, 0, "s")
+        regroup_w(1, 0, "v")
+        for g in range(2):
+            for b in range(2):
+                agg_out(0, g, b, "s")
+        quantise_w(0, 0)
+        quantise_w(1, 0)
+        quantise_agg(0, 0)
+        quantise_agg(0, 1)
+        agg_out(1, 0, 0, "s")
+        agg_out(1, 0, 1, "s")
+        quantise_agg(1, 0)
+        for j in range(4):
+            layer_pass(j, 0)
+        agg_out(1, 1, 0, "s")
+        agg_out(1, 1, 1, "s")
+        regroup_w(0, 1, "v")
+        quantise_agg(1, 1)
+        for j in range(4):
+            layer_pass(j, 1)
+        regroup_w(1, 1, "v")
+        quantise_w(0, 1)
+        quantise_w(1, 1)
+        for j in range(4):
+            scale_shift(j, "s")
+        for j in range(4, 8):
+            layer_pass(j, 0)
+            layer_pass(j, 1)
+        for i in range(4):
+            turn_back(i, 0)
+        for j in range(4, 8):
+            scale_shift(j, "s" if j % 2 else "v")
+        for i in range(4):
+            relu_store(i, 0, "s" if i % 2 else "v")
+        for i in range(4):
+            turn_back(i, 1)
+        for i in range(4):
+            relu_store(i, 1, "s" if i % 2 else "v")

@@ -56,10 +56,6 @@ def tile_bipartitegcnstack_pb_kernel(
 
         vec_rows = keep.tile([P, P], BF16, name="vec_rows")
         nc.vector.memset(vec_rows[:], 0.0)
-        for v, vec in enumerate((bb0, bn_b_gamma, bn_b_beta, bn_b_mean, bn_b_var)):
-            nc.scalar.dma_start(
-                out=vec_rows[8 * v : 8 * v + 8, :], in_=vec.rearrange("(r c) -> r c", c=P)
-            )
         for c in range(2):
             nc.sync.dma_start(
                 out=a_raw[c][:],
@@ -74,6 +70,10 @@ def tile_bipartitegcnstack_pb_kernel(
             nc.sync.dma_start(
                 out=w_raw[f][:], in_=Wb0[:, 512 * f : 512 * (f + 1)].rearrange("(r p) o -> p r o", p=P)
             )
+        for v, vec in enumerate((bb0, bn_b_gamma, bn_b_beta, bn_b_mean, bn_b_var)):
+            nc.sync.dma_start(
+                out=vec_rows[8 * v : 8 * v + 8, :], in_=vec.rearrange("(r c) -> r c", c=P)
+            )
         warm_in = keep.tile([P, 1], F32, name="warm_in")
         nc.vector.memset(warm_in[:], 1.0)
         warm_out = keep.tile([P, 1], F32, name="warm_out")
@@ -85,24 +85,33 @@ def tile_bipartitegcnstack_pb_kernel(
         ident_b = keep.tile([P, P], BF16, name="ident_b")
         nc.vector.tensor_copy(out=ident_b[:], in_=ident_f[:])
 
-        vec_ps = psum.tile([P, P], BF16, tag="bank", name="vec_ps")
-        nc.tensor.transpose(vec_ps[:], vec_rows[:], ident_b[:])
         vec_t = keep.tile([P, 40], F32, name="vec_t")
-        nc.vector.tensor_copy(out=vec_t[:], in_=vec_ps[:, 0:40])
         var_eps = keep.tile([P, 8], F32, name="var_eps")
-        nc.vector.tensor_scalar_add(out=var_eps[:], in0=vec_t[:, 32:40], scalar1=EPS_BN)
         std = keep.tile([P, 8], F32, name="std")
-        nc.scalar.sqrt(out=std[:], in_=var_eps[:])
         rstd = keep.tile([P, 8], F32, name="rstd")
-        nc.vector.reciprocal(out=rstd[:], in_=std[:])
         sc = keep.tile([P, 8], F32, name="sc")
-        nc.vector.tensor_tensor(out=sc[:], in0=vec_t[:, 8:16], in1=rstd[:], op=ALU.mult)
         diff = keep.tile([P, 8], F32, name="diff")
-        nc.vector.tensor_tensor(out=diff[:], in0=vec_t[:, 0:8], in1=vec_t[:, 24:32], op=ALU.subtract)
         prod = keep.tile([P, 8], F32, name="prod")
-        nc.vector.tensor_tensor(out=prod[:], in0=diff[:], in1=sc[:], op=ALU.mult)
         sh = keep.tile([P, 8], F32, name="sh")
-        nc.vector.tensor_tensor(out=sh[:], in0=prod[:], in1=vec_t[:, 16:24], op=ALU.add)
+        vec_ps = {}
+
+        def bn_transpose():
+            vec_ps[0] = psum.tile([P, P], BF16, tag="bank", name="vec_ps")
+            nc.tensor.transpose(vec_ps[0][:], vec_rows[:], ident_b[:])
+
+        def bn_copy():
+            nc.scalar.copy(out=vec_t[:], in_=vec_ps[0][:, 0:40])
+            nc.gpsimd.tensor_scalar_add(out=var_eps[:], in0=vec_t[:, 32:40], scalar1=EPS_BN)
+            nc.gpsimd.tensor_tensor(out=diff[:], in0=vec_t[:, 0:8], in1=vec_t[:, 24:32], op=ALU.subtract)
+
+        def bn_sqrt():
+            nc.scalar.sqrt(out=std[:], in_=var_eps[:])
+
+        def bn_finish():
+            nc.vector.reciprocal(out=rstd[:], in_=std[:])
+            nc.gpsimd.tensor_tensor(out=sc[:], in0=vec_t[:, 8:16], in1=rstd[:], op=ALU.mult)
+            nc.gpsimd.tensor_tensor(out=prod[:], in0=diff[:], in1=sc[:], op=ALU.mult)
+            nc.gpsimd.tensor_tensor(out=sh[:], in0=prod[:], in1=vec_t[:, 16:24], op=ALU.add)
 
         cs_ps = psum.tile([P, 2, 4, 64], F32, tag="bank", name="cs_ps")
         for c in range(2):
@@ -251,6 +260,7 @@ def tile_bipartitegcnstack_pb_kernel(
         quantise_h(1, 1)
         agg_block(0, 1, 0)
         agg_block(0, 1, 1)
+        bn_transpose()
         normalise_a(0, 1)
         normalise_a(1, 1)
         quantise_a(1)
@@ -259,11 +269,15 @@ def tile_bipartitegcnstack_pb_kernel(
                 agg_block(1, g, b)
         regroup_w(0, 0, "s")
         regroup_w(1, 0, "v")
-        for g in range(2):
-            for b in range(2):
-                agg_out(0, g, b, "s")
+        agg_out(0, 0, 0, "s")
+        bn_copy()
+        agg_out(0, 0, 1, "s")
+        agg_out(0, 1, 0, "s")
+        agg_out(0, 1, 1, "s")
+        bn_sqrt()
         quantise_w(0, 0)
         quantise_w(1, 0)
+        bn_finish()
         quantise_agg(0, 0)
         quantise_agg(0, 1)
         agg_out(1, 0, 0, "s")
@@ -274,24 +288,24 @@ def tile_bipartitegcnstack_pb_kernel(
         agg_out(1, 1, 0, "s")
         agg_out(1, 1, 1, "s")
         regroup_w(0, 1, "v")
+        regroup_w(1, 1, "s")
         quantise_agg(1, 1)
         for j in range(4):
             layer_pass(j, 1)
-        regroup_w(1, 1, "v")
         quantise_w(0, 1)
         quantise_w(1, 1)
         for j in range(4):
-            scale_shift(j, "s")
+            scale_shift(j, "v" if j % 2 else "s")
         for j in range(4, 8):
             layer_pass(j, 0)
             layer_pass(j, 1)
         for i in range(4):
             turn_back(i, 0)
         for j in range(4, 8):
-            scale_shift(j, "s" if j % 2 else "v")
+            scale_shift(j, "v" if j % 2 else "s")
         for i in range(4):
-            relu_store(i, 0, "s" if i % 2 else "v")
+            relu_store(i, 0, "v" if i % 2 else "s")
         for i in range(4):
             turn_back(i, 1)
         for i in range(4):
-            relu_store(i, 1, "s" if i % 2 else "v")
+            relu_store(i, 1, "v" if i % 2 else "s")

@@ -17,6 +17,7 @@ PACK = 4
 K_PASS = P * PACK
 NS, NT, DH, DB = 512, 1024, 1024, 1024
 HALF = 256
+N_WARM = 6
 EPS_ROW = 1e-8
 EPS_BN = 1e-5
 FLOPS = 2 * NS * NT * DH + 2 * NS * DH * DB
@@ -54,6 +55,13 @@ def tile_bipartitegcnstack_pb_kernel(
         g_scales = keep.tile([P, 2, NS], U8, name="g_scales", align_bytes=64)
         y_t = [keep.tile([P, NS], F32, name="y_t%d" % j) for j in range(8)]
 
+        ones = keep.tile([P, P], BF16, name="ones")
+        nc.vector.memset(ones[:], 1.0)
+        warm_rhs = keep.tile([P, 512], BF16, name="warm_rhs")
+        nc.vector.memset(warm_rhs[:], 0.0)
+        warm_ps = psum.tile([P, 512], F32, tag="bank", name="warm_ps")
+        for n in range(N_WARM):
+            nc.tensor.matmul(out=warm_ps[:], lhsT=ones[:], rhs=warm_rhs[:], start=True, stop=True)
         vec_rows = keep.tile([P, P], BF16, name="vec_rows")
         nc.vector.memset(vec_rows[:], 0.0)
         for c in range(2):
@@ -80,8 +88,6 @@ def tile_bipartitegcnstack_pb_kernel(
         nc.scalar.sqrt(out=warm_out[:], in_=warm_in[:])
         ident_f = keep.tile([P, P], F32, name="ident_f")
         make_identity(nc, ident_f[:])
-        ones = keep.tile([P, 64], BF16, name="ones")
-        nc.vector.memset(ones[:], 1.0)
         ident_b = keep.tile([P, P], BF16, name="ident_b")
         nc.vector.tensor_copy(out=ident_b[:], in_=ident_f[:])
 
@@ -120,7 +126,7 @@ def tile_bipartitegcnstack_pb_kernel(
                     nc.tensor.matmul(
                         out=cs_ps[:, c, i, :],
                         lhsT=a_raw[c][:, j, P * i : P * (i + 1)],
-                        rhs=ones[:],
+                        rhs=ones[:, 0:64],
                         start=(j == 0),
                         stop=(j == PACK - 1),
                     )

@@ -17,7 +17,6 @@ PACK = 4
 K_PASS = P * PACK
 NS, NT, DH, DB = 512, 1024, 1024, 1024
 HALF = 256
-N_WARM = 6
 EPS_ROW = 1e-8
 EPS_BN = 1e-5
 FLOPS = 2 * NS * NT * DH + 2 * NS * DH * DB
@@ -30,7 +29,6 @@ def tile_bipartitegcnstack_pb_kernel(
     with ExitStack() as ctx:
         keep = ctx.enter_context(tc.tile_pool(name="keep", bufs=1))
         psum = ctx.enter_context(tc.psum_pool(name="psum", bufs=8))
-        ctx.enter_context(tc.manual_schedule())
 
         copies = {"v": nc.vector.tensor_copy, "s": nc.scalar.copy}
 
@@ -55,13 +53,6 @@ def tile_bipartitegcnstack_pb_kernel(
         g_scales = keep.tile([P, 2, NS], U8, name="g_scales", align_bytes=64)
         y_t = [keep.tile([P, NS], F32, name="y_t%d" % j) for j in range(8)]
 
-        ones = keep.tile([P, P], BF16, name="ones")
-        nc.vector.memset(ones[:], 1.0)
-        warm_rhs = keep.tile([P, 512], BF16, name="warm_rhs")
-        nc.vector.memset(warm_rhs[:], 0.0)
-        warm_ps = psum.tile([P, 512], F32, tag="bank", name="warm_ps")
-        for n in range(N_WARM):
-            nc.tensor.matmul(out=warm_ps[:], lhsT=ones[:], rhs=warm_rhs[:], start=True, stop=True)
         vec_rows = keep.tile([P, P], BF16, name="vec_rows")
         nc.vector.memset(vec_rows[:], 0.0)
         for c in range(2):
@@ -88,6 +79,8 @@ def tile_bipartitegcnstack_pb_kernel(
         nc.scalar.sqrt(out=warm_out[:], in_=warm_in[:])
         ident_f = keep.tile([P, P], F32, name="ident_f")
         make_identity(nc, ident_f[:])
+        ones = keep.tile([P, 64], BF16, name="ones")
+        nc.vector.memset(ones[:], 1.0)
         ident_b = keep.tile([P, P], BF16, name="ident_b")
         nc.vector.tensor_copy(out=ident_b[:], in_=ident_f[:])
 
@@ -126,7 +119,7 @@ def tile_bipartitegcnstack_pb_kernel(
                     nc.tensor.matmul(
                         out=cs_ps[:, c, i, :],
                         lhsT=a_raw[c][:, j, P * i : P * (i + 1)],
-                        rhs=ones[:, 0:64],
+                        rhs=ones[:],
                         start=(j == 0),
                         stop=(j == PACK - 1),
                     )

@@ -29,6 +29,7 @@ def tile_bipartitegcnstack_pb_kernel(
     with ExitStack() as ctx:
         keep = ctx.enter_context(tc.tile_pool(name="keep", bufs=1))
         psum = ctx.enter_context(tc.psum_pool(name="psum", bufs=8))
+        ctx.enter_context(tc.manual_schedule())
 
         copies = {"v": nc.vector.tensor_copy, "s": nc.scalar.copy}
 
@@ -65,16 +66,19 @@ def tile_bipartitegcnstack_pb_kernel(
                 out=h_raw[c][:],
                 in_=h_tgt[K_PASS * c : K_PASS * (c + 1), :].rearrange("(p j) d -> p j d", j=PACK),
             )
-        for f in range(2):
-            nc.sync.dma_start(
-                out=w_raw[f][:], in_=Wb0[:, 512 * f : 512 * (f + 1)].rearrange("(r p) o -> p r o", p=P)
-            )
         for v, vec in enumerate((bb0, bn_b_gamma, bn_b_beta, bn_b_mean, bn_b_var)):
             nc.sync.dma_start(
                 out=vec_rows[8 * v : 8 * v + 8, :], in_=vec.rearrange("(r c) -> r c", c=P)
             )
+        for f in range(2):
+            nc.sync.dma_start(
+                out=w_raw[f][:], in_=Wb0[:, 512 * f : 512 * (f + 1)].rearrange("(r p) o -> p r o", p=P)
+            )
         warm_in = keep.tile([P, 1], F32, name="warm_in")
         nc.vector.memset(warm_in[:], 1.0)
+        eps_bn = keep.tile([P, 1], F32, name="eps_bn")
+        nc.vector.memset(eps_bn[:], EPS_BN)
+        gate = keep.tile([P, 1], F32, name="gate")
         warm_out = keep.tile([P, 1], F32, name="warm_out")
         nc.scalar.sqrt(out=warm_out[:], in_=warm_in[:])
         ident_f = keep.tile([P, P], F32, name="ident_f")
@@ -85,7 +89,6 @@ def tile_bipartitegcnstack_pb_kernel(
         nc.vector.tensor_copy(out=ident_b[:], in_=ident_f[:])
 
         vec_t = keep.tile([P, 40], F32, name="vec_t")
-        var_eps = keep.tile([P, 8], F32, name="var_eps")
         std = keep.tile([P, 8], F32, name="std")
         rstd = keep.tile([P, 8], F32, name="rstd")
         sc = keep.tile([P, 8], F32, name="sc")
@@ -100,11 +103,8 @@ def tile_bipartitegcnstack_pb_kernel(
 
         def bn_copy():
             nc.scalar.copy(out=vec_t[:], in_=vec_ps[0][:, 0:40])
-            nc.gpsimd.tensor_scalar_add(out=var_eps[:], in0=vec_t[:, 32:40], scalar1=EPS_BN)
+            nc.scalar.activation(out=std[:], in_=vec_ps[0][:, 32:40], func=ACT.Sqrt, bias=eps_bn[:, 0:1])
             nc.gpsimd.tensor_tensor(out=diff[:], in0=vec_t[:, 0:8], in1=vec_t[:, 24:32], op=ALU.subtract)
-
-        def bn_sqrt():
-            nc.scalar.sqrt(out=std[:], in_=var_eps[:])
 
         def bn_finish():
             nc.vector.reciprocal(out=rstd[:], in_=std[:])
@@ -148,6 +148,13 @@ def tile_bipartitegcnstack_pb_kernel(
 
         def regroup_h(c, g, eng):
             regroup(eng, h_grp[(c, g)][:], h_raw[c][:, :, 512 * g : 512 * (g + 1)])
+
+        def regroup_h_gpsimd(c, g):
+            nc.gpsimd.tensor_scalar(
+                out=h_grp[(c, g)][:],
+                in0=h_raw[c][:, :, 512 * g : 512 * (g + 1)].rearrange("p j w -> p w j"),
+                scalar1=gate[:, 0:1], scalar2=0.0, op0=ALU.mult, op1=ALU.add,
+            )
 
         def quantise_h(c, g):
             cols = slice(512 * g, 512 * (g + 1))
@@ -244,39 +251,38 @@ def tile_bipartitegcnstack_pb_kernel(
                 nc.vector.tensor_scalar_max(out=o_sb[:], in0=o_ps[(i, f)][:], scalar1=0.0)
             nc.sync.dma_start(out=out[P * i : P * (i + 1), 512 * f : 512 * (f + 1)], in_=o_sb[:])
 
+        bn_transpose()
         regroup_h(0, 0, "v")
+        nc.vector.memset(gate[:], 1.0)
         regroup_h(0, 1, "s")
-        normalise_a(0, 0)
-        normalise_a(1, 0)
         regroup_h(1, 0, "s")
-        regroup_h(1, 1, "s")
+        regroup_h_gpsimd(1, 1)
+        bn_copy()
+        for hh in range(2):
+            normalise_a(0, hh)
+            normalise_a(1, hh)
+        bn_finish()
         quantise_h(0, 0)
-        quantise_a(0)
         quantise_h(1, 0)
+        quantise_a(0)
         agg_block(0, 0, 0)
         agg_block(0, 0, 1)
         quantise_h(0, 1)
         quantise_h(1, 1)
+        quantise_a(1)
         agg_block(0, 1, 0)
         agg_block(0, 1, 1)
-        bn_transpose()
-        normalise_a(0, 1)
-        normalise_a(1, 1)
-        quantise_a(1)
         for g in range(2):
             for b in range(2):
                 agg_block(1, g, b)
         regroup_w(0, 0, "s")
-        regroup_w(1, 0, "v")
-        agg_out(0, 0, 0, "s")
-        bn_copy()
-        agg_out(0, 0, 1, "s")
-        agg_out(0, 1, 0, "s")
-        agg_out(0, 1, 1, "s")
-        bn_sqrt()
+        regroup_w(1, 0, "s")
         quantise_w(0, 0)
         quantise_w(1, 0)
-        bn_finish()
+        for g in range(2):
+            for b in range(2):
+                agg_out(0, g, b, "s")
+        regroup_w(0, 1, "v")
         quantise_agg(0, 0)
         quantise_agg(0, 1)
         agg_out(1, 0, 0, "s")
@@ -284,19 +290,21 @@ def tile_bipartitegcnstack_pb_kernel(
         quantise_agg(1, 0)
         for j in range(4):
             layer_pass(j, 0)
+        quantise_w(0, 1)
         agg_out(1, 1, 0, "s")
         agg_out(1, 1, 1, "s")
-        regroup_w(0, 1, "v")
-        regroup_w(1, 1, "s")
         quantise_agg(1, 1)
         for j in range(4):
             layer_pass(j, 1)
-        quantise_w(0, 1)
-        quantise_w(1, 1)
-        for j in range(4):
-            scale_shift(j, "v" if j % 2 else "s")
+        regroup_w(1, 1, "v")
         for j in range(4, 8):
             layer_pass(j, 0)
+        quantise_w(1, 1)
+        scale_shift(0, "s")
+        scale_shift(1, "s")
+        scale_shift(2, "s")
+        scale_shift(3, "v")
+        for j in range(4, 8):
             layer_pass(j, 1)
         for i in range(4):
             turn_back(i, 0)

@@ -258,20 +258,21 @@ def tile_bipartitegcnstack_pb_kernel(
         regroup_h(1, 0, "s")
         regroup_h_gpsimd(1, 1)
         bn_copy()
-        for hh in range(2):
-            normalise_a(0, hh)
-            normalise_a(1, hh)
-        bn_finish()
+        normalise_a(0, 0)
+        normalise_a(1, 0)
+        normalise_a(0, 1)
+        quantise_a(0)
         quantise_h(0, 0)
         quantise_h(1, 0)
-        quantise_a(0)
         agg_block(0, 0, 0)
         agg_block(0, 0, 1)
         quantise_h(0, 1)
         quantise_h(1, 1)
-        quantise_a(1)
         agg_block(0, 1, 0)
         agg_block(0, 1, 1)
+        bn_finish()
+        normalise_a(1, 1)
+        quantise_a(1)
         for g in range(2):
             for b in range(2):
                 agg_block(1, g, b)

@@ -10,7 +10,6 @@ U32 = mybir.dt.uint32
 U8 = mybir.dt.uint8
 ALU = mybir.AluOpType
 ACT = mybir.ActivationFunctionType
-AX = mybir.AxisListType
 
 P = 128
 PACK = 4
@@ -33,17 +32,22 @@ def tile_bipartitegcnstack_pb_kernel(
 
         copies = {"v": nc.vector.tensor_copy, "s": nc.scalar.copy}
 
-        a_raw = [keep.tile([P, PACK, NS], BF16, name="a_raw%d" % c) for c in range(2)]
-        h_raw = [keep.tile([P, PACK, DH], BF16, name="h_raw%d" % c) for c in range(2)]
-        w_raw = [keep.tile([P, 2 * PACK, 512], BF16, name="w_raw%d" % f) for f in range(2)]
-        a_grp = [keep.tile([P, 2, HALF, PACK], BF16, name="a_grp%d" % hh, align_bytes=64) for hh in range(2)]
-        g_grp = [keep.tile([P, NS, PACK], BF16, name="g_grp%d" % g, align_bytes=64) for g in range(2)]
+        a_raw = {}
+        for hh in range(2):
+            for c in range(2):
+                a_raw[(hh, c)] = keep.tile([P, PACK, HALF], BF16, name="a_raw%d%d" % (hh, c))
+        h_raw = {}
         h_grp = {}
+        w_raw = {}
         w_grp = {}
         for x in range(2):
             for y in range(2):
+                h_raw[(x, y)] = keep.tile([P, PACK, 512], BF16, name="h_raw%d%d" % (x, y))
                 h_grp[(x, y)] = keep.tile([P, 512, PACK], BF16, name="h_grp%d%d" % (x, y), align_bytes=64)
+                w_raw[(x, y)] = keep.tile([P, PACK, 512], BF16, name="w_raw%d%d" % (x, y))
                 w_grp[(x, y)] = keep.tile([P, 512, PACK], BF16, name="w_grp%d%d" % (x, y), align_bytes=64)
+        a_grp = [keep.tile([P, 2, HALF, PACK], BF16, name="a_grp%d" % hh, align_bytes=64) for hh in range(2)]
+        g_grp = [keep.tile([P, NS, PACK], BF16, name="g_grp%d" % g, align_bytes=64) for g in range(2)]
         a_codes = [keep.tile([P, 2 * HALF], U32, name="a_codes%d" % hh, align_bytes=64) for hh in range(2)]
         a_scales = [keep.tile([P, 2 * HALF], U8, name="a_scales%d" % hh, align_bytes=64) for hh in range(2)]
         h_codes = keep.tile([P, 2, DH], U32, name="h_codes", align_bytes=64)
@@ -53,38 +57,57 @@ def tile_bipartitegcnstack_pb_kernel(
         g_codes = keep.tile([P, 2, NS], U32, name="g_codes", align_bytes=64)
         g_scales = keep.tile([P, 2, NS], U8, name="g_scales", align_bytes=64)
         y_t = [keep.tile([P, NS], F32, name="y_t%d" % j) for j in range(8)]
-
         vec_rows = keep.tile([P, P], BF16, name="vec_rows")
         nc.vector.memset(vec_rows[:], 0.0)
-        for c in range(2):
+
+        def load_a(hh, c):
             nc.sync.dma_start(
-                out=a_raw[c][:],
-                in_=A[K_PASS * c : K_PASS * (c + 1), :].rearrange("(p j) s -> p j s", j=PACK),
+                out=a_raw[(hh, c)][:],
+                in_=A[K_PASS * c : K_PASS * (c + 1), HALF * hh : HALF * (hh + 1)].rearrange("(p j) s -> p j s", j=PACK),
             )
-        for c in range(2):
+
+        def load_h(c, g):
             nc.sync.dma_start(
-                out=h_raw[c][:],
-                in_=h_tgt[K_PASS * c : K_PASS * (c + 1), :].rearrange("(p j) d -> p j d", j=PACK),
+                out=h_raw[(c, g)][:],
+                in_=h_tgt[K_PASS * c : K_PASS * (c + 1), 512 * g : 512 * (g + 1)].rearrange("(p j) d -> p j d", j=PACK),
             )
-        for v, vec in enumerate((bb0, bn_b_gamma, bn_b_beta, bn_b_mean, bn_b_var)):
+
+        def load_w(g, f):
             nc.sync.dma_start(
-                out=vec_rows[8 * v : 8 * v + 8, :], in_=vec.rearrange("(r c) -> r c", c=P)
+                out=w_raw[(g, f)][:],
+                in_=Wb0[K_PASS * g : K_PASS * (g + 1), 512 * f : 512 * (f + 1)].rearrange("(r p) o -> p r o", p=P),
             )
-        for f in range(2):
-            nc.sync.dma_start(
-                out=w_raw[f][:], in_=Wb0[:, 512 * f : 512 * (f + 1)].rearrange("(r p) o -> p r o", p=P)
-            )
+
+        def load_vecs():
+            for v, vec in enumerate((bb0, bn_b_gamma, bn_b_beta, bn_b_mean, bn_b_var)):
+                nc.sync.dma_start(
+                    out=vec_rows[8 * v : 8 * v + 8, :], in_=vec.rearrange("(r c) -> r c", c=P)
+                )
+
+        load_a(0, 0)
+        load_a(0, 1)
+        load_h(0, 0)
+        load_h(0, 1)
+        load_a(1, 0)
+        load_a(1, 1)
+        load_h(1, 0)
+        load_h(1, 1)
+        load_vecs()
+        load_w(0, 0)
+        load_w(1, 0)
+        load_w(0, 1)
+        load_w(1, 1)
+
         warm_in = keep.tile([P, 1], F32, name="warm_in")
         nc.vector.memset(warm_in[:], 1.0)
+        ones = keep.tile([P, 8], BF16, name="ones")
+        nc.vector.memset(ones[:], 1.0)
         eps_bn = keep.tile([P, 1], F32, name="eps_bn")
         nc.vector.memset(eps_bn[:], EPS_BN)
-        gate = keep.tile([P, 1], F32, name="gate")
         warm_out = keep.tile([P, 1], F32, name="warm_out")
         nc.scalar.sqrt(out=warm_out[:], in_=warm_in[:])
         ident_f = keep.tile([P, P], F32, name="ident_f")
         make_identity(nc, ident_f[:])
-        ones = keep.tile([P, 64], BF16, name="ones")
-        nc.vector.memset(ones[:], 1.0)
         ident_b = keep.tile([P, P], BF16, name="ident_b")
         nc.vector.tensor_copy(out=ident_b[:], in_=ident_f[:])
 
@@ -112,30 +135,36 @@ def tile_bipartitegcnstack_pb_kernel(
             nc.gpsimd.tensor_tensor(out=prod[:], in0=diff[:], in1=sc[:], op=ALU.mult)
             nc.gpsimd.tensor_tensor(out=sh[:], in0=prod[:], in1=vec_t[:, 16:24], op=ALU.add)
 
-        cs_ps = psum.tile([P, 2, 4, 64], F32, tag="bank", name="cs_ps")
-        for c in range(2):
-            for i in range(4):
-                for j in range(PACK):
-                    nc.tensor.matmul(
-                        out=cs_ps[:, c, i, :],
-                        lhsT=a_raw[c][:, j, P * i : P * (i + 1)],
-                        rhs=ones[:],
-                        start=(j == 0),
-                        stop=(j == PACK - 1),
-                    )
-        cs = keep.tile([P, 4], F32, name="cs")
-        nc.vector.tensor_reduce(
-            out=cs[:], in_=cs_ps[:, :, :, 0].rearrange("p c i -> p i c"), axis=AX.X, op=ALU.add
-        )
+        cs_ps = {}
         cs_cl = keep.tile([P, 4], F32, name="cs_cl")
-        nc.vector.tensor_scalar_max(out=cs_cl[:], in0=cs[:], scalar1=EPS_ROW)
         rec = keep.tile([P, 4], F32, name="rec")
-        nc.vector.reciprocal(out=rec[:], in_=cs_cl[:])
-        rec_rep = keep.tile([P, 4, P], F32, name="rec_rep")
-        nc.vector.tensor_copy(out=rec_rep[:], in_=rec[:].unsqueeze(2).to_broadcast([P, 4, P]))
-        r_bc = psum.tile([P, NS], F32, tag="bank", name="r_bc")
-        for i in range(4):
-            nc.tensor.transpose(r_bc[:, P * i : P * (i + 1)], rec_rep[:, i, :], ident_f[:])
+        r_bc = {}
+
+        def column_sums(hh):
+            cs_ps[hh] = psum.tile([P, 2, 8], F32, tag="bank", name="cs_ps")
+            for b in range(2):
+                for c in range(2):
+                    for j in range(PACK):
+                        nc.tensor.matmul(
+                            out=cs_ps[hh][:, b, :],
+                            lhsT=a_raw[(hh, c)][:, j, P * b : P * (b + 1)],
+                            rhs=ones[:],
+                            start=(c == 0 and j == 0),
+                            stop=(c == 1 and j == PACK - 1),
+                        )
+
+        def reciprocals(hh):
+            cols = slice(2 * hh, 2 * hh + 2)
+            nc.vector.tensor_scalar_max(out=cs_cl[:, cols], in0=cs_ps[hh][:, :, 0], scalar1=EPS_ROW)
+            nc.vector.reciprocal(out=rec[:, cols], in_=cs_cl[:, cols])
+
+        def spread(hh):
+            r_bc[hh] = psum.tile([P, HALF], F32, tag="bank", name="r_bc")
+            for b in range(2):
+                i = 2 * hh + b
+                nc.tensor.transpose(
+                    r_bc[hh][:, P * b : P * (b + 1)], rec[:, i : i + 1].to_broadcast([P, P]), ident_f[:]
+                )
 
         def regroup(eng, dst, src):
             copies[eng](
@@ -146,33 +175,72 @@ def tile_bipartitegcnstack_pb_kernel(
         def quantise(codes, scales, grouped):
             nc.vector.quantize_mx(out=codes.bitcast(FP8X4), scales=scales, in_=grouped)
 
-        def regroup_h(c, g, eng):
-            regroup(eng, h_grp[(c, g)][:], h_raw[c][:, :, 512 * g : 512 * (g + 1)])
+        def regroup_h(c, g, lo, hi, eng):
+            regroup(eng, h_grp[(c, g)][:, lo:hi, :], h_raw[(c, g)][:, :, lo:hi])
 
-        def regroup_h_gpsimd(c, g):
-            nc.gpsimd.tensor_scalar(
-                out=h_grp[(c, g)][:],
-                in0=h_raw[c][:, :, 512 * g : 512 * (g + 1)].rearrange("p j w -> p w j"),
-                scalar1=gate[:, 0:1], scalar2=0.0, op0=ALU.mult, op1=ALU.add,
+        perm = {}
+
+        def permute_h(c, g, u):
+            bank = psum.tile([P, 2, 512], BF16, tag="bank", name="perm")
+            perm[(c, g, u)] = bank
+            for v in range(2):
+                w0 = 256 * u + 128 * v
+                nc.tensor.matmul(
+                    out=bank[:, v, :].rearrange("p (w j) -> p w j", j=PACK),
+                    lhsT=ident_b[:],
+                    rhs=h_raw[(c, g)][:, :, w0 : w0 + 128].rearrange("p j w -> p w j"),
+                    start=True,
+                    stop=True,
+                )
+
+        def take_h(c, g, u):
+            nc.scalar.copy(
+                out=h_grp[(c, g)][:, 256 * u : 256 * (u + 1), :].rearrange("p w j -> p (w j)"),
+                in_=perm[(c, g, u)][:].rearrange("p v n -> p (v n)"),
             )
 
         def quantise_h(c, g):
             cols = slice(512 * g, 512 * (g + 1))
             quantise(h_codes[:, c, cols], h_scales[:, c, cols], h_grp[(c, g)][:].rearrange("p w j -> p (w j)"))
 
-        def regroup_w(g, f, eng):
-            regroup(eng, w_grp[(g, f)][:], w_raw[f][:, PACK * g : PACK * (g + 1), :])
+        def regroup_w(g, f, lo, hi, eng):
+            regroup(eng, w_grp[(g, f)][:, lo:hi, :], w_raw[(g, f)][:, :, lo:hi])
 
-        def quantise_w(g, f):
-            cols = slice(512 * f, 512 * (f + 1))
-            quantise(w_codes[:, g, cols], w_scales[:, g, cols], w_grp[(g, f)][:].rearrange("p w j -> p (w j)"))
+        def regroup_w_gpsimd(g, f, lo, hi):
+            nc.gpsimd.tensor_scalar(
+                out=w_grp[(g, f)][:, lo:hi, :],
+                in0=w_raw[(g, f)][:, :, lo:hi].rearrange("p j w -> p w j"),
+                scalar1=1.0, scalar2=0.0, op0=ALU.mult, op1=ALU.add,
+            )
+
+        def permute_w(g, f, u):
+            bank = psum.tile([P, 2, 512], BF16, tag="bank", name="perm")
+            perm[("w", g, f, u)] = bank
+            for v in range(2):
+                w0 = 256 * u + 128 * v
+                nc.tensor.matmul(
+                    out=bank[:, v, :].rearrange("p (w j) -> p w j", j=PACK),
+                    lhsT=ident_b[:],
+                    rhs=w_raw[(g, f)][:, :, w0 : w0 + 128].rearrange("p j w -> p w j"),
+                    start=True,
+                    stop=True,
+                )
+
+        def take_w(g, f, u):
+            nc.scalar.copy(
+                out=w_grp[(g, f)][:, 256 * u : 256 * (u + 1), :].rearrange("p w j -> p (w j)"),
+                in_=perm[("w", g, f, u)][:].rearrange("p v n -> p (v n)"),
+            )
+
+        def quantise_w(g, f, lo, hi):
+            cols = slice(512 * f + lo, 512 * f + hi)
+            quantise(w_codes[:, g, cols], w_scales[:, g, cols], w_grp[(g, f)][:, lo:hi, :].rearrange("p w j -> p (w j)"))
 
         def normalise_a(c, hh):
-            cols = slice(HALF * hh, HALF * (hh + 1))
             nc.vector.tensor_tensor(
                 out=a_grp[hh][:, c].rearrange("p (q i) j -> p q j i", i=4),
-                in0=a_raw[c][:, :, cols].rearrange("p j (q i) -> p q j i", i=4),
-                in1=r_bc[:, cols].rearrange("p (q i) -> p q i", i=4).unsqueeze(2).to_broadcast([P, HALF // 4, PACK, 4]),
+                in0=a_raw[(hh, c)][:].rearrange("p j (q i) -> p q j i", i=4),
+                in1=r_bc[hh][:].rearrange("p (q i) -> p q i", i=4).unsqueeze(2).to_broadcast([P, HALF // 4, PACK, 4]),
                 op=ALU.mult,
             )
 
@@ -208,29 +276,30 @@ def tile_bipartitegcnstack_pb_kernel(
 
         h_ps = {}
 
-        def layer_pass(j, g):
-            if g == 0:
-                h_ps[j] = psum.tile([P, NS], F32, tag="bank", name="h_ps")
+        def layer(hh, j):
+            if j % 2 == 0:
+                h_ps[(hh, j // 2)] = psum.tile([P, 2, HALF], F32, tag="bank", name="h_ps")
             o_cols = slice(P * j, P * (j + 1))
-            nc.tensor.matmul_mx(
-                out=h_ps[j][:],
-                lhsT=w_codes[:, g, o_cols].bitcast(FP8X4),
-                lhsT_scale=w_scales[:, g, o_cols],
-                rhs=g_codes[:, g, :].bitcast(FP8X4),
-                rhs_scale=g_scales[:, g, :],
-                start=(g == 0),
-                stop=(g == 1),
-            )
-
-        def scale_shift(j, eng):
-            if eng == "s":
-                nc.scalar.activation(
-                    out=y_t[j][:], in_=h_ps[j][:], func=ACT.Identity, bias=sh[:, j : j + 1], scale=sc[:, j : j + 1]
+            s_cols = slice(HALF * hh, HALF * (hh + 1))
+            for g in range(2):
+                nc.tensor.matmul_mx(
+                    out=h_ps[(hh, j // 2)][:, j % 2, :],
+                    lhsT=w_codes[:, g, o_cols].bitcast(FP8X4),
+                    lhsT_scale=w_scales[:, g, o_cols],
+                    rhs=g_codes[:, g, s_cols].bitcast(FP8X4),
+                    rhs_scale=g_scales[:, g, s_cols],
+                    start=(g == 0),
+                    stop=(g == 1),
                 )
+
+        def scale_shift(hh, j, eng):
+            y = y_t[j][:, HALF * hh : HALF * (hh + 1)]
+            x = h_ps[(hh, j // 2)][:, j % 2, :]
+            if eng == "s":
+                nc.scalar.activation(out=y, in_=x, func=ACT.Identity, bias=sh[:, j : j + 1], scale=sc[:, j : j + 1])
             else:
                 nc.vector.tensor_scalar(
-                    out=y_t[j][:], in0=h_ps[j][:], scalar1=sc[:, j : j + 1], scalar2=sh[:, j : j + 1],
-                    op0=ALU.mult, op1=ALU.add,
+                    out=y, in0=x, scalar1=sc[:, j : j + 1], scalar2=sh[:, j : j + 1], op0=ALU.mult, op1=ALU.add
                 )
 
         o_ps = {}
@@ -251,69 +320,106 @@ def tile_bipartitegcnstack_pb_kernel(
                 nc.vector.tensor_scalar_max(out=o_sb[:], in0=o_ps[(i, f)][:], scalar1=0.0)
             nc.sync.dma_start(out=out[P * i : P * (i + 1), 512 * f : 512 * (f + 1)], in_=o_sb[:])
 
-        bn_transpose()
-        regroup_h(0, 0, "v")
-        nc.vector.memset(gate[:], 1.0)
-        regroup_h(0, 1, "s")
-        regroup_h(1, 0, "s")
-        regroup_h_gpsimd(1, 1)
-        bn_copy()
+        column_sums(0)
+        reciprocals(0)
+        regroup_h(0, 0, 0, 256, "v")
+        regroup_h(0, 0, 256, 512, "s")
+        spread(0)
+        regroup_h(0, 1, 0, 512, "s")
         normalise_a(0, 0)
         normalise_a(1, 0)
-        normalise_a(0, 1)
+        column_sums(1)
+        permute_h(1, 0, 0)
+        permute_h(1, 0, 1)
+        reciprocals(1)
+        spread(1)
         quantise_a(0)
         quantise_h(0, 0)
+        quantise_h(0, 1)
+        take_h(1, 0, 0)
+        take_h(1, 0, 1)
+        permute_h(1, 1, 0)
+        permute_h(1, 1, 1)
         quantise_h(1, 0)
+        take_h(1, 1, 0)
+        take_h(1, 1, 1)
+        normalise_a(0, 1)
+        regroup_w_gpsimd(0, 0, 0, 256)
+        permute_w(0, 0, 1)
         agg_block(0, 0, 0)
         agg_block(0, 0, 1)
-        quantise_h(0, 1)
         quantise_h(1, 1)
+        normalise_a(1, 1)
+        permute_w(1, 0, 0)
+        agg_out(0, 0, 0, "s")
+        take_w(0, 0, 1)
         agg_block(0, 1, 0)
         agg_block(0, 1, 1)
-        bn_finish()
-        normalise_a(1, 1)
+        bn_transpose()
+        agg_out(0, 0, 1, "s")
+        take_w(1, 0, 0)
         quantise_a(1)
-        for g in range(2):
-            for b in range(2):
-                agg_block(1, g, b)
-        regroup_w(0, 0, "s")
-        regroup_w(1, 0, "s")
-        quantise_w(0, 0)
-        quantise_w(1, 0)
-        for g in range(2):
-            for b in range(2):
-                agg_out(0, g, b, "s")
-        regroup_w(0, 1, "v")
+        agg_out(0, 1, 0, "s")
+        agg_out(0, 1, 1, "s")
+        bn_copy()
+        agg_block(1, 0, 0)
+        agg_block(1, 0, 1)
+        agg_block(1, 1, 0)
+        agg_block(1, 1, 1)
+        regroup_w(1, 0, 256, 512, "v")
+        quantise_w(0, 0, 0, 512)
+        bn_finish()
+        quantise_w(1, 0, 0, 512)
         quantise_agg(0, 0)
         quantise_agg(0, 1)
         agg_out(1, 0, 0, "s")
         agg_out(1, 0, 1, "s")
-        quantise_agg(1, 0)
         for j in range(4):
-            layer_pass(j, 0)
-        quantise_w(0, 1)
+            layer(0, j)
         agg_out(1, 1, 0, "s")
         agg_out(1, 1, 1, "s")
+        regroup_w(0, 1, 0, 256, "v")
+        quantise_agg(1, 0)
         quantise_agg(1, 1)
+        regroup_w(0, 1, 256, 512, "v")
         for j in range(4):
-            layer_pass(j, 1)
-        regroup_w(1, 1, "v")
-        for j in range(4, 8):
-            layer_pass(j, 0)
-        quantise_w(1, 1)
-        scale_shift(0, "s")
-        scale_shift(1, "s")
-        scale_shift(2, "s")
-        scale_shift(3, "v")
-        for j in range(4, 8):
-            layer_pass(j, 1)
-        for i in range(4):
+            layer(1, j)
+        for j in range(4):
+            scale_shift(0, j, "s")
+        for i in range(2):
             turn_back(i, 0)
-        for j in range(4, 8):
-            scale_shift(j, "v" if j % 2 else "s")
-        for i in range(4):
+        quantise_w(0, 1, 0, 512)
+        regroup_w(1, 1, 0, 256, "v")
+        for j in range(4):
+            scale_shift(1, j, "s")
+        for i in range(2, 4):
+            turn_back(i, 0)
+        quantise_w(1, 1, 0, 256)
+        regroup_w(1, 1, 256, 512, "v")
+        for i in range(2):
+            relu_store(i, 0, "s")
+        for hh in range(2):
+            for j in range(4, 6):
+                layer(hh, j)
+        quantise_w(1, 1, 256, 512)
+        for j in range(4, 6):
+            scale_shift(0, j, "v")
+        for j in range(4, 6):
+            scale_shift(1, j, "s")
+        for hh in range(2):
+            for j in range(6, 8):
+                layer(hh, j)
+        for i in range(2, 4):
             relu_store(i, 0, "v" if i % 2 else "s")
-        for i in range(4):
+        for j in range(6, 8):
+            scale_shift(0, j, "v")
+        for j in range(6, 8):
+            scale_shift(1, j, "s")
+        for i in range(2):
             turn_back(i, 1)
-        for i in range(4):
+        for i in range(2):
+            relu_store(i, 1, "v" if i % 2 else "s")
+        for i in range(2, 4):
+            turn_back(i, 1)
+        for i in range(2, 4):
             relu_store(i, 1, "v" if i % 2 else "s")

@@ -178,27 +178,6 @@ def tile_bipartitegcnstack_pb_kernel(
         def regroup_h(c, g, lo, hi, eng):
             regroup(eng, h_grp[(c, g)][:, lo:hi, :], h_raw[(c, g)][:, :, lo:hi])
 
-        perm = {}
-
-        def permute_h(c, g, u):
-            bank = psum.tile([P, 2, 512], BF16, tag="bank", name="perm")
-            perm[(c, g, u)] = bank
-            for v in range(2):
-                w0 = 256 * u + 128 * v
-                nc.tensor.matmul(
-                    out=bank[:, v, :].rearrange("p (w j) -> p w j", j=PACK),
-                    lhsT=ident_b[:],
-                    rhs=h_raw[(c, g)][:, :, w0 : w0 + 128].rearrange("p j w -> p w j"),
-                    start=True,
-                    stop=True,
-                )
-
-        def take_h(c, g, u):
-            nc.scalar.copy(
-                out=h_grp[(c, g)][:, 256 * u : 256 * (u + 1), :].rearrange("p w j -> p (w j)"),
-                in_=perm[(c, g, u)][:].rearrange("p v n -> p (v n)"),
-            )
-
         def quantise_h(c, g):
             cols = slice(512 * g, 512 * (g + 1))
             quantise(h_codes[:, c, cols], h_scales[:, c, cols], h_grp[(c, g)][:].rearrange("p w j -> p (w j)"))
@@ -211,25 +190,6 @@ def tile_bipartitegcnstack_pb_kernel(
                 out=w_grp[(g, f)][:, lo:hi, :],
                 in0=w_raw[(g, f)][:, :, lo:hi].rearrange("p j w -> p w j"),
                 scalar1=1.0, scalar2=0.0, op0=ALU.mult, op1=ALU.add,
-            )
-
-        def permute_w(g, f, u):
-            bank = psum.tile([P, 2, 512], BF16, tag="bank", name="perm")
-            perm[("w", g, f, u)] = bank
-            for v in range(2):
-                w0 = 256 * u + 128 * v
-                nc.tensor.matmul(
-                    out=bank[:, v, :].rearrange("p (w j) -> p w j", j=PACK),
-                    lhsT=ident_b[:],
-                    rhs=w_raw[(g, f)][:, :, w0 : w0 + 128].rearrange("p j w -> p w j"),
-                    start=True,
-                    stop=True,
-                )
-
-        def take_w(g, f, u):
-            nc.scalar.copy(
-                out=w_grp[(g, f)][:, 256 * u : 256 * (u + 1), :].rearrange("p w j -> p (w j)"),
-                in_=perm[("w", g, f, u)][:].rearrange("p v n -> p (v n)"),
             )
 
         def quantise_w(g, f, lo, hi):
@@ -329,35 +289,29 @@ def tile_bipartitegcnstack_pb_kernel(
         normalise_a(0, 0)
         normalise_a(1, 0)
         column_sums(1)
-        permute_h(1, 0, 0)
-        permute_h(1, 0, 1)
         reciprocals(1)
         spread(1)
         quantise_a(0)
         quantise_h(0, 0)
         quantise_h(0, 1)
-        take_h(1, 0, 0)
-        take_h(1, 0, 1)
-        permute_h(1, 1, 0)
-        permute_h(1, 1, 1)
+        regroup_h(1, 0, 0, 256, "s")
+        regroup_h(1, 0, 256, 512, "s")
         quantise_h(1, 0)
-        take_h(1, 1, 0)
-        take_h(1, 1, 1)
+        regroup_h(1, 1, 0, 256, "s")
+        regroup_h(1, 1, 256, 512, "s")
         normalise_a(0, 1)
         regroup_w_gpsimd(0, 0, 0, 256)
-        permute_w(0, 0, 1)
         agg_block(0, 0, 0)
         agg_block(0, 0, 1)
         quantise_h(1, 1)
         normalise_a(1, 1)
-        permute_w(1, 0, 0)
         agg_out(0, 0, 0, "s")
-        take_w(0, 0, 1)
+        regroup_w(0, 0, 256, 512, "s")
         agg_block(0, 1, 0)
         agg_block(0, 1, 1)
         bn_transpose()
         agg_out(0, 0, 1, "s")
-        take_w(1, 0, 0)
+        regroup_w(1, 0, 0, 256, "s")
         quantise_a(1)
         agg_out(0, 1, 0, "s")
         agg_out(0, 1, 1, "s")

@@ -32,17 +32,13 @@ def tile_bipartitegcnstack_pb_kernel(
 
         copies = {"v": nc.vector.tensor_copy, "s": nc.scalar.copy}
 
-        a_raw = {}
-        for hh in range(2):
-            for c in range(2):
-                a_raw[(hh, c)] = keep.tile([P, PACK, HALF], BF16, name="a_raw%d%d" % (hh, c))
-        h_raw = {}
+        a_raw = [keep.tile([P, PACK, NS], BF16, name="a_raw%d" % c) for c in range(2)]
+        h_raw = [keep.tile([P, PACK, DH], BF16, name="h_raw%d" % c) for c in range(2)]
         h_grp = {}
         w_raw = {}
         w_grp = {}
         for x in range(2):
             for y in range(2):
-                h_raw[(x, y)] = keep.tile([P, PACK, 512], BF16, name="h_raw%d%d" % (x, y))
                 h_grp[(x, y)] = keep.tile([P, 512, PACK], BF16, name="h_grp%d%d" % (x, y), align_bytes=64)
                 w_raw[(x, y)] = keep.tile([P, PACK, 512], BF16, name="w_raw%d%d" % (x, y))
                 w_grp[(x, y)] = keep.tile([P, 512, PACK], BF16, name="w_grp%d%d" % (x, y), align_bytes=64)
@@ -60,16 +56,14 @@ def tile_bipartitegcnstack_pb_kernel(
         vec_rows = keep.tile([P, P], BF16, name="vec_rows")
         nc.vector.memset(vec_rows[:], 0.0)
 
-        def load_a(hh, c):
+        def load_a(c):
             nc.sync.dma_start(
-                out=a_raw[(hh, c)][:],
-                in_=A[K_PASS * c : K_PASS * (c + 1), HALF * hh : HALF * (hh + 1)].rearrange("(p j) s -> p j s", j=PACK),
+                out=a_raw[c][:], in_=A[K_PASS * c : K_PASS * (c + 1), :].rearrange("(p j) s -> p j s", j=PACK)
             )
 
-        def load_h(c, g):
+        def load_h(c):
             nc.sync.dma_start(
-                out=h_raw[(c, g)][:],
-                in_=h_tgt[K_PASS * c : K_PASS * (c + 1), 512 * g : 512 * (g + 1)].rearrange("(p j) d -> p j d", j=PACK),
+                out=h_raw[c][:], in_=h_tgt[K_PASS * c : K_PASS * (c + 1), :].rearrange("(p j) d -> p j d", j=PACK)
             )
 
         def load_w(g, f):
@@ -84,14 +78,10 @@ def tile_bipartitegcnstack_pb_kernel(
                     out=vec_rows[8 * v : 8 * v + 8, :], in_=vec.rearrange("(r c) -> r c", c=P)
                 )
 
-        load_a(0, 0)
-        load_a(0, 1)
-        load_h(0, 0)
-        load_h(0, 1)
-        load_a(1, 0)
-        load_a(1, 1)
-        load_h(1, 0)
-        load_h(1, 1)
+        load_a(0)
+        load_a(1)
+        load_h(0)
+        load_h(1)
         load_vecs()
         load_w(0, 0)
         load_w(1, 0)
@@ -104,6 +94,7 @@ def tile_bipartitegcnstack_pb_kernel(
         nc.vector.memset(ones[:], 1.0)
         eps_bn = keep.tile([P, 1], F32, name="eps_bn")
         nc.vector.memset(eps_bn[:], EPS_BN)
+        one = keep.tile([P, 1], F32, name="one")
         warm_out = keep.tile([P, 1], F32, name="warm_out")
         nc.scalar.sqrt(out=warm_out[:], in_=warm_in[:])
         ident_f = keep.tile([P, P], F32, name="ident_f")
@@ -147,7 +138,7 @@ def tile_bipartitegcnstack_pb_kernel(
                     for j in range(PACK):
                         nc.tensor.matmul(
                             out=cs_ps[hh][:, b, :],
-                            lhsT=a_raw[(hh, c)][:, j, P * b : P * (b + 1)],
+                            lhsT=a_raw[c][:, j, HALF * hh + P * b : HALF * hh + P * (b + 1)],
                             rhs=ones[:],
                             start=(c == 0 and j == 0),
                             stop=(c == 1 and j == PACK - 1),
@@ -176,11 +167,18 @@ def tile_bipartitegcnstack_pb_kernel(
             nc.vector.quantize_mx(out=codes.bitcast(FP8X4), scales=scales, in_=grouped)
 
         def regroup_h(c, g, lo, hi, eng):
-            regroup(eng, h_grp[(c, g)][:, lo:hi, :], h_raw[(c, g)][:, :, lo:hi])
+            regroup(eng, h_grp[(c, g)][:, lo:hi, :], h_raw[c][:, :, 512 * g + lo : 512 * g + hi])
 
         def quantise_h(c, g):
             cols = slice(512 * g, 512 * (g + 1))
             quantise(h_codes[:, c, cols], h_scales[:, c, cols], h_grp[(c, g)][:].rearrange("p w j -> p (w j)"))
+
+        def regroup_h_gpsimd(c, g, lo, hi):
+            nc.gpsimd.tensor_scalar(
+                out=h_grp[(c, g)][:, lo:hi, :],
+                in0=h_raw[c][:, :, 512 * g + lo : 512 * g + hi].rearrange("p j w -> p w j"),
+                scalar1=one[:, 0:1], scalar2=0.0, op0=ALU.mult, op1=ALU.add,
+            )
 
         def regroup_w(g, f, lo, hi, eng):
             regroup(eng, w_grp[(g, f)][:, lo:hi, :], w_raw[(g, f)][:, :, lo:hi])
@@ -199,7 +197,7 @@ def tile_bipartitegcnstack_pb_kernel(
         def normalise_a(c, hh):
             nc.vector.tensor_tensor(
                 out=a_grp[hh][:, c].rearrange("p (q i) j -> p q j i", i=4),
-                in0=a_raw[(hh, c)][:].rearrange("p j (q i) -> p q j i", i=4),
+                in0=a_raw[c][:, :, HALF * hh : HALF * (hh + 1)].rearrange("p j (q i) -> p q j i", i=4),
                 in1=r_bc[hh][:].rearrange("p (q i) -> p q i", i=4).unsqueeze(2).to_broadcast([P, HALF // 4, PACK, 4]),
                 op=ALU.mult,
             )
@@ -281,50 +279,46 @@ def tile_bipartitegcnstack_pb_kernel(
             nc.sync.dma_start(out=out[P * i : P * (i + 1), 512 * f : 512 * (f + 1)], in_=o_sb[:])
 
         column_sums(0)
-        reciprocals(0)
-        regroup_h(0, 0, 0, 256, "v")
-        regroup_h(0, 0, 256, 512, "s")
-        spread(0)
-        regroup_h(0, 1, 0, 512, "s")
-        normalise_a(0, 0)
-        normalise_a(1, 0)
         column_sums(1)
+        reciprocals(0)
+        spread(0)
         reciprocals(1)
         spread(1)
-        quantise_a(0)
-        quantise_h(0, 0)
-        quantise_h(0, 1)
-        regroup_h(1, 0, 0, 256, "s")
-        regroup_h(1, 0, 256, 512, "s")
-        quantise_h(1, 0)
-        regroup_h(1, 1, 0, 256, "s")
-        regroup_h(1, 1, 256, 512, "s")
+        regroup_h(0, 0, 0, 512, "s")
+        normalise_a(0, 0)
+        nc.vector.memset(one[:], 1.0)
+        normalise_a(1, 0)
+        regroup_h_gpsimd(0, 1, 0, 512)
+        regroup_h(1, 0, 0, 512, "s")
         normalise_a(0, 1)
-        regroup_w_gpsimd(0, 0, 0, 256)
+        normalise_a(1, 1)
+        quantise_h(0, 0)
+        quantise_a(0)
+        regroup_h(1, 1, 256, 512, "s")
+        bn_transpose()
+        bn_copy()
+        regroup_h(1, 1, 0, 256, "v")
+        regroup_w(0, 0, 0, 512, "s")
+        quantise_h(1, 0)
         agg_block(0, 0, 0)
         agg_block(0, 0, 1)
+        quantise_h(0, 1)
         quantise_h(1, 1)
-        normalise_a(1, 1)
-        agg_out(0, 0, 0, "s")
-        regroup_w(0, 0, 256, 512, "s")
         agg_block(0, 1, 0)
         agg_block(0, 1, 1)
-        bn_transpose()
-        agg_out(0, 0, 1, "s")
-        regroup_w(1, 0, 0, 256, "s")
         quantise_a(1)
-        agg_out(0, 1, 0, "s")
-        agg_out(0, 1, 1, "s")
-        bn_copy()
+        bn_finish()
         agg_block(1, 0, 0)
         agg_block(1, 0, 1)
         agg_block(1, 1, 0)
         agg_block(1, 1, 1)
-        regroup_w(1, 0, 256, 512, "v")
+        for g in range(2):
+            for b in range(2):
+                agg_out(0, g, b, "s")
+        regroup_w(1, 0, 0, 512, "v")
         quantise_w(0, 0, 0, 512)
-        bn_finish()
-        quantise_w(1, 0, 0, 512)
         quantise_agg(0, 0)
+        quantise_w(1, 0, 0, 512)
         quantise_agg(0, 1)
         agg_out(1, 0, 0, "s")
         agg_out(1, 0, 1, "s")

@@ -35,12 +35,11 @@ def tile_bipartitegcnstack_pb_kernel(
         a_raw = [keep.tile([P, PACK, NS], BF16, name="a_raw%d" % c) for c in range(2)]
         h_raw = [keep.tile([P, PACK, DH], BF16, name="h_raw%d" % c) for c in range(2)]
         h_grp = {}
-        w_raw = {}
+        w_raw = [keep.tile([P, PACK, DB], BF16, name="w_raw%d" % g) for g in range(2)]
         w_grp = {}
         for x in range(2):
             for y in range(2):
                 h_grp[(x, y)] = keep.tile([P, 512, PACK], BF16, name="h_grp%d%d" % (x, y), align_bytes=64)
-                w_raw[(x, y)] = keep.tile([P, PACK, 512], BF16, name="w_raw%d%d" % (x, y))
                 w_grp[(x, y)] = keep.tile([P, 512, PACK], BF16, name="w_grp%d%d" % (x, y), align_bytes=64)
         a_grp = [keep.tile([P, 2, HALF, PACK], BF16, name="a_grp%d" % hh, align_bytes=64) for hh in range(2)]
         g_grp = [keep.tile([P, NS, PACK], BF16, name="g_grp%d" % g, align_bytes=64) for g in range(2)]
@@ -66,10 +65,9 @@ def tile_bipartitegcnstack_pb_kernel(
                 out=h_raw[c][:], in_=h_tgt[K_PASS * c : K_PASS * (c + 1), :].rearrange("(p j) d -> p j d", j=PACK)
             )
 
-        def load_w(g, f):
+        def load_w(g):
             nc.sync.dma_start(
-                out=w_raw[(g, f)][:],
-                in_=Wb0[K_PASS * g : K_PASS * (g + 1), 512 * f : 512 * (f + 1)].rearrange("(r p) o -> p r o", p=P),
+                out=w_raw[g][:], in_=Wb0[K_PASS * g : K_PASS * (g + 1), :].rearrange("(r p) o -> p r o", p=P)
             )
 
         def load_vecs():
@@ -83,10 +81,8 @@ def tile_bipartitegcnstack_pb_kernel(
         load_h(0)
         load_h(1)
         load_vecs()
-        load_w(0, 0)
-        load_w(1, 0)
-        load_w(0, 1)
-        load_w(1, 1)
+        load_w(0)
+        load_w(1)
 
         warm_in = keep.tile([P, 1], F32, name="warm_in")
         nc.vector.memset(warm_in[:], 1.0)
@@ -181,14 +177,7 @@ def tile_bipartitegcnstack_pb_kernel(
             )
 
         def regroup_w(g, f, lo, hi, eng):
-            regroup(eng, w_grp[(g, f)][:, lo:hi, :], w_raw[(g, f)][:, :, lo:hi])
-
-        def regroup_w_gpsimd(g, f, lo, hi):
-            nc.gpsimd.tensor_scalar(
-                out=w_grp[(g, f)][:, lo:hi, :],
-                in0=w_raw[(g, f)][:, :, lo:hi].rearrange("p j w -> p w j"),
-                scalar1=1.0, scalar2=0.0, op0=ALU.mult, op1=ALU.add,
-            )
+            regroup(eng, w_grp[(g, f)][:, lo:hi, :], w_raw[g][:, :, 512 * f + lo : 512 * f + hi])
 
         def quantise_w(g, f, lo, hi):
             cols = slice(512 * f + lo, 512 * f + hi)

@@ -80,9 +80,9 @@ def tile_bipartitegcnstack_pb_kernel(
         load_a(1)
         load_h(0)
         load_h(1)
-        load_vecs()
         load_w(0)
         load_w(1)
+        load_vecs()
 
         warm_in = keep.tile([P, 1], F32, name="warm_in")
         nc.vector.memset(warm_in[:], 1.0)
@@ -114,35 +114,37 @@ def tile_bipartitegcnstack_pb_kernel(
         def bn_copy():
             nc.scalar.copy(out=vec_t[:], in_=vec_ps[0][:, 0:40])
             nc.scalar.activation(out=std[:], in_=vec_ps[0][:, 32:40], func=ACT.Sqrt, bias=eps_bn[:, 0:1])
-            nc.gpsimd.tensor_tensor(out=diff[:], in0=vec_t[:, 0:8], in1=vec_t[:, 24:32], op=ALU.subtract)
 
-        def bn_finish():
-            nc.vector.reciprocal(out=rstd[:], in_=std[:])
-            nc.gpsimd.tensor_tensor(out=sc[:], in0=vec_t[:, 8:16], in1=rstd[:], op=ALU.mult)
-            nc.gpsimd.tensor_tensor(out=prod[:], in0=diff[:], in1=sc[:], op=ALU.mult)
-            nc.gpsimd.tensor_tensor(out=sh[:], in0=prod[:], in1=vec_t[:, 16:24], op=ALU.add)
+        def bn_step(k):
+            if k == 0:
+                nc.vector.reciprocal(out=rstd[:], in_=std[:])
+                nc.vector.tensor_tensor(out=diff[:], in0=vec_t[:, 0:8], in1=vec_t[:, 24:32], op=ALU.subtract)
+            elif k == 1:
+                nc.vector.tensor_tensor(out=sc[:], in0=vec_t[:, 8:16], in1=rstd[:], op=ALU.mult)
+            elif k == 2:
+                nc.vector.tensor_tensor(out=prod[:], in0=diff[:], in1=sc[:], op=ALU.mult)
+            else:
+                nc.vector.tensor_tensor(out=sh[:], in0=prod[:], in1=vec_t[:, 16:24], op=ALU.add)
 
-        cs_ps = {}
+        cs_ps = [psum.tile([P, 8], F32, tag="bank", name="cs_ps%d" % i) for i in range(4)]
         cs_cl = keep.tile([P, 4], F32, name="cs_cl")
         rec = keep.tile([P, 4], F32, name="rec")
         r_bc = {}
 
-        def column_sums(hh):
-            cs_ps[hh] = psum.tile([P, 2, 8], F32, tag="bank", name="cs_ps")
-            for b in range(2):
-                for c in range(2):
-                    for j in range(PACK):
-                        nc.tensor.matmul(
-                            out=cs_ps[hh][:, b, :],
-                            lhsT=a_raw[c][:, j, HALF * hh + P * b : HALF * hh + P * (b + 1)],
-                            rhs=ones[:],
-                            start=(c == 0 and j == 0),
-                            stop=(c == 1 and j == PACK - 1),
-                        )
+        def column_sums(c, i):
+            for j in range(PACK):
+                nc.tensor.matmul(
+                    out=cs_ps[i][:],
+                    lhsT=a_raw[c][:, j, P * i : P * (i + 1)],
+                    rhs=ones[:],
+                    start=(c == 0 and j == 0),
+                    stop=(c == 1 and j == PACK - 1),
+                )
 
         def reciprocals(hh):
             cols = slice(2 * hh, 2 * hh + 2)
-            nc.vector.tensor_scalar_max(out=cs_cl[:, cols], in0=cs_ps[hh][:, :, 0], scalar1=EPS_ROW)
+            for i in range(2 * hh, 2 * hh + 2):
+                nc.vector.tensor_scalar_max(out=cs_cl[:, i : i + 1], in0=cs_ps[i][:, 0:1], scalar1=EPS_ROW)
             nc.vector.reciprocal(out=rec[:, cols], in_=cs_cl[:, cols])
 
         def spread(hh):
@@ -267,36 +269,35 @@ def tile_bipartitegcnstack_pb_kernel(
                 nc.vector.tensor_scalar_max(out=o_sb[:], in0=o_ps[(i, f)][:], scalar1=0.0)
             nc.sync.dma_start(out=out[P * i : P * (i + 1), 512 * f : 512 * (f + 1)], in_=o_sb[:])
 
-        column_sums(0)
-        column_sums(1)
+        for c in range(2):
+            for i in range(4):
+                column_sums(c, i)
         reciprocals(0)
-        spread(0)
         reciprocals(1)
+        spread(0)
         spread(1)
         regroup_h(0, 0, 0, 512, "s")
-        normalise_a(0, 0)
         nc.vector.memset(one[:], 1.0)
+        normalise_a(0, 0)
         normalise_a(1, 0)
         regroup_h_gpsimd(0, 1, 0, 512)
         regroup_h(1, 0, 0, 512, "s")
         normalise_a(0, 1)
-        normalise_a(1, 1)
         quantise_h(0, 0)
         quantise_a(0)
-        regroup_h(1, 1, 256, 512, "s")
-        bn_transpose()
-        bn_copy()
         regroup_h(1, 1, 0, 256, "v")
-        regroup_w(0, 0, 0, 512, "s")
+        regroup_h(1, 1, 256, 512, "s")
         quantise_h(1, 0)
         agg_block(0, 0, 0)
         agg_block(0, 0, 1)
         quantise_h(0, 1)
+        normalise_a(1, 1)
+        regroup_w(0, 0, 0, 512, "s")
         quantise_h(1, 1)
         agg_block(0, 1, 0)
         agg_block(0, 1, 1)
+        bn_transpose()
         quantise_a(1)
-        bn_finish()
         agg_block(1, 0, 0)
         agg_block(1, 0, 1)
         agg_block(1, 1, 0)
@@ -304,59 +305,59 @@ def tile_bipartitegcnstack_pb_kernel(
         for g in range(2):
             for b in range(2):
                 agg_out(0, g, b, "s")
+        bn_copy()
         regroup_w(1, 0, 0, 512, "v")
         quantise_w(0, 0, 0, 512)
         quantise_agg(0, 0)
         quantise_w(1, 0, 0, 512)
+        bn_step(0)
         quantise_agg(0, 1)
+        bn_step(1)
         agg_out(1, 0, 0, "s")
         agg_out(1, 0, 1, "s")
         for j in range(4):
             layer(0, j)
         agg_out(1, 1, 0, "s")
         agg_out(1, 1, 1, "s")
-        regroup_w(0, 1, 0, 256, "v")
+        regroup_w(0, 1, 0, 512, "v")
+        bn_step(2)
         quantise_agg(1, 0)
+        bn_step(3)
         quantise_agg(1, 1)
-        regroup_w(0, 1, 256, 512, "v")
+        regroup_w(1, 1, 0, 256, "v")
         for j in range(4):
             layer(1, j)
         for j in range(4):
             scale_shift(0, j, "s")
+        quantise_w(0, 1, 0, 512)
         for i in range(2):
             turn_back(i, 0)
-        quantise_w(0, 1, 0, 512)
-        regroup_w(1, 1, 0, 256, "v")
+        regroup_w(1, 1, 256, 512, "v")
         for j in range(4):
             scale_shift(1, j, "s")
+        quantise_w(1, 1, 0, 256)
         for i in range(2, 4):
             turn_back(i, 0)
-        quantise_w(1, 1, 0, 256)
-        regroup_w(1, 1, 256, 512, "v")
-        for i in range(2):
-            relu_store(i, 0, "s")
+        quantise_w(1, 1, 256, 512)
         for hh in range(2):
             for j in range(4, 6):
                 layer(hh, j)
-        quantise_w(1, 1, 256, 512)
-        for j in range(4, 6):
-            scale_shift(0, j, "v")
-        for j in range(4, 6):
-            scale_shift(1, j, "s")
         for hh in range(2):
             for j in range(6, 8):
                 layer(hh, j)
-        for i in range(2, 4):
-            relu_store(i, 0, "v" if i % 2 else "s")
+        relu_store(0, 0, "s")
+        relu_store(1, 0, "v")
+        for j in range(4, 6):
+            scale_shift(0, j, "v")
+        for j in range(4, 6):
+            scale_shift(1, j, "s")
+        relu_store(2, 0, "s")
+        relu_store(3, 0, "v")
         for j in range(6, 8):
             scale_shift(0, j, "v")
         for j in range(6, 8):
             scale_shift(1, j, "s")
-        for i in range(2):
+        for i in range(4):
             turn_back(i, 1)
-        for i in range(2):
-            relu_store(i, 1, "v" if i % 2 else "s")
-        for i in range(2, 4):
-            turn_back(i, 1)
-        for i in range(2, 4):
+        for i in range(4):
             relu_store(i, 1, "v" if i % 2 else "s")

@@ -43,14 +43,14 @@ def tile_bipartitegcnstack_pb_kernel(
                 w_grp[(x, y)] = keep.tile([P, 512, PACK], BF16, name="w_grp%d%d" % (x, y), align_bytes=64)
         a_grp = [keep.tile([P, 2, HALF, PACK], BF16, name="a_grp%d" % hh, align_bytes=64) for hh in range(2)]
         g_grp = [keep.tile([P, NS, PACK], BF16, name="g_grp%d" % g, align_bytes=64) for g in range(2)]
-        a_codes = [keep.tile([P, 2 * HALF], U32, name="a_codes%d" % hh, align_bytes=64) for hh in range(2)]
-        a_scales = [keep.tile([P, 2 * HALF], U8, name="a_scales%d" % hh, align_bytes=64) for hh in range(2)]
-        h_codes = keep.tile([P, 2, DH], U32, name="h_codes", align_bytes=64)
-        h_scales = keep.tile([P, 2, DH], U8, name="h_scales", align_bytes=64)
-        w_codes = keep.tile([P, 2, DB], U32, name="w_codes", align_bytes=64)
-        w_scales = keep.tile([P, 2, DB], U8, name="w_scales", align_bytes=64)
-        g_codes = keep.tile([P, 2, NS], U32, name="g_codes", align_bytes=64)
-        g_scales = keep.tile([P, 2, NS], U8, name="g_scales", align_bytes=64)
+        a_codes = [keep.tile([P, 2 * HALF], U32, name="a_codes%d" % hh, align_bytes=256) for hh in range(2)]
+        a_scales = [keep.tile([P, 2 * HALF], U8, name="a_scales%d" % hh, align_bytes=256) for hh in range(2)]
+        h_codes = keep.tile([P, 2, DH], U32, name="h_codes", align_bytes=256)
+        h_scales = keep.tile([P, 2, DH], U8, name="h_scales", align_bytes=256)
+        w_codes = keep.tile([P, 2, DB], U32, name="w_codes", align_bytes=256)
+        w_scales = keep.tile([P, 2, DB], U8, name="w_scales", align_bytes=256)
+        g_codes = keep.tile([P, 2, NS], U32, name="g_codes", align_bytes=256)
+        g_scales = keep.tile([P, 2, NS], U8, name="g_scales", align_bytes=256)
         y_t = [keep.tile([P, NS], F32, name="y_t%d" % j) for j in range(8)]
         vec_rows = keep.tile([P, P], BF16, name="vec_rows")
         nc.vector.memset(vec_rows[:], 0.0)

@@ -80,9 +80,9 @@ def tile_bipartitegcnstack_pb_kernel(
         load_a(1)
         load_h(0)
         load_h(1)
+        load_vecs()
         load_w(0)
         load_w(1)
-        load_vecs()
 
         warm_in = keep.tile([P, 1], F32, name="warm_in")
         nc.vector.memset(warm_in[:], 1.0)
@@ -276,6 +276,7 @@ def tile_bipartitegcnstack_pb_kernel(
         reciprocals(1)
         spread(0)
         spread(1)
+        bn_transpose()
         regroup_h(0, 0, 0, 512, "s")
         nc.vector.memset(one[:], 1.0)
         normalise_a(0, 0)
@@ -287,17 +288,20 @@ def tile_bipartitegcnstack_pb_kernel(
         quantise_a(0)
         regroup_h(1, 1, 0, 256, "v")
         regroup_h(1, 1, 256, 512, "s")
+        bn_copy()
         quantise_h(1, 0)
         agg_block(0, 0, 0)
         agg_block(0, 0, 1)
         quantise_h(0, 1)
         normalise_a(1, 1)
+        bn_step(0)
         regroup_w(0, 0, 0, 512, "s")
         quantise_h(1, 1)
+        bn_step(1)
         agg_block(0, 1, 0)
         agg_block(0, 1, 1)
-        bn_transpose()
         quantise_a(1)
+        bn_step(2)
         agg_block(1, 0, 0)
         agg_block(1, 0, 1)
         agg_block(1, 1, 0)
@@ -305,14 +309,12 @@ def tile_bipartitegcnstack_pb_kernel(
         for g in range(2):
             for b in range(2):
                 agg_out(0, g, b, "s")
-        bn_copy()
         regroup_w(1, 0, 0, 512, "v")
+        bn_step(3)
         quantise_w(0, 0, 0, 512)
         quantise_agg(0, 0)
         quantise_w(1, 0, 0, 512)
-        bn_step(0)
         quantise_agg(0, 1)
-        bn_step(1)
         agg_out(1, 0, 0, "s")
         agg_out(1, 0, 1, "s")
         for j in range(4):
@@ -320,9 +322,7 @@ def tile_bipartitegcnstack_pb_kernel(
         agg_out(1, 1, 0, "s")
         agg_out(1, 1, 1, "s")
         regroup_w(0, 1, 0, 512, "v")
-        bn_step(2)
         quantise_agg(1, 0)
-        bn_step(3)
         quantise_agg(1, 1)
         regroup_w(1, 1, 0, 256, "v")
         for j in range(4):
@@ -336,28 +336,26 @@ def tile_bipartitegcnstack_pb_kernel(
         for j in range(4):
             scale_shift(1, j, "s")
         quantise_w(1, 1, 0, 256)
+        quantise_w(1, 1, 256, 512)
         for i in range(2, 4):
             turn_back(i, 0)
-        quantise_w(1, 1, 256, 512)
-        for hh in range(2):
-            for j in range(4, 6):
-                layer(hh, j)
-        for hh in range(2):
-            for j in range(6, 8):
-                layer(hh, j)
+        for j in range(4, 8):
+            layer(0, j)
+        for j in range(4, 8):
+            layer(1, j)
         relu_store(0, 0, "s")
         relu_store(1, 0, "v")
-        for j in range(4, 6):
-            scale_shift(0, j, "v")
-        for j in range(4, 6):
-            scale_shift(1, j, "s")
         relu_store(2, 0, "s")
         relu_store(3, 0, "v")
-        for j in range(6, 8):
-            scale_shift(0, j, "v")
-        for j in range(6, 8):
-            scale_shift(1, j, "s")
-        for i in range(4):
+        for j in range(4, 8):
+            scale_shift(0, j, "v" if j < 6 else "s")
+        for i in range(2):
             turn_back(i, 1)
-        for i in range(4):
+        for j in range(4, 8):
+            scale_shift(1, j, "v" if j < 6 else "s")
+        for i in range(2):
+            relu_store(i, 1, "v" if i % 2 else "s")
+        for i in range(2, 4):
+            turn_back(i, 1)
+        for i in range(2, 4):
             relu_store(i, 1, "v" if i % 2 else "s")

from contextlib import ExitStack

import concourse.mybir as mybir
from concourse.masks import make_identity

FP8X4 = mybir.dt.float8_e4m3fn_x4
BF16 = mybir.dt.bfloat16
F32 = mybir.dt.float32
U32 = mybir.dt.uint32
U8 = mybir.dt.uint8
ALU = mybir.AluOpType
ACT = mybir.ActivationFunctionType

P = 128
PACK = 4
K_PASS = P * PACK
NS, NT, DH, DB = 512, 1024, 1024, 1024
HALF = 256
EPS_ROW = 1e-8
EPS_BN = 1e-5
FLOPS = 2 * NS * NT * DH + 2 * NS * DH * DB


def tile_bipartitegcnstack_pb_kernel(
    tc, h_tgt, A, Wb0, bb0, bn_b_gamma, bn_b_beta, bn_b_mean, bn_b_var, out
):
    nc = tc.nc
    with ExitStack() as ctx:
        keep = ctx.enter_context(tc.tile_pool(name="keep", bufs=1))
        psum = ctx.enter_context(tc.psum_pool(name="psum", bufs=8))
        ctx.enter_context(tc.manual_schedule())

        copies = {"v": nc.vector.tensor_copy, "s": nc.scalar.copy}

        a_raw = [keep.tile([P, PACK, NS], BF16, name="a_raw%d" % c) for c in range(2)]
        h_raw = [keep.tile([P, PACK, DH], BF16, name="h_raw%d" % c) for c in range(2)]
        h_grp = {}
        w_raw = [keep.tile([P, PACK, DB], BF16, name="w_raw%d" % g) for g in range(2)]
        w_grp = {}
        for x in range(2):
            for y in range(2):
                h_grp[(x, y)] = keep.tile([P, 512, PACK], BF16, name="h_grp%d%d" % (x, y), align_bytes=64)
                w_grp[(x, y)] = keep.tile([P, 512, PACK], BF16, name="w_grp%d%d" % (x, y), align_bytes=64)
        a_grp = [keep.tile([P, 2, HALF, PACK], BF16, name="a_grp%d" % hh, align_bytes=64) for hh in range(2)]
        g_grp = [keep.tile([P, NS, PACK], BF16, name="g_grp%d" % g, align_bytes=64) for g in range(2)]
        a_codes = [keep.tile([P, 2 * HALF], U32, name="a_codes%d" % hh, align_bytes=256) for hh in range(2)]
        a_scales = [keep.tile([P, 2 * HALF], U8, name="a_scales%d" % hh, align_bytes=256) for hh in range(2)]
        h_codes = keep.tile([P, 2, DH], U32, name="h_codes", align_bytes=256)
        h_scales = keep.tile([P, 2, DH], U8, name="h_scales", align_bytes=256)
        w_codes = keep.tile([P, 2, DB], U32, name="w_codes", align_bytes=256)
        w_scales = keep.tile([P, 2, DB], U8, name="w_scales", align_bytes=256)
        g_codes = keep.tile([P, 2, NS], U32, name="g_codes", align_bytes=256)
        g_scales = keep.tile([P, 2, NS], U8, name="g_scales", align_bytes=256)
        y_t = [keep.tile([P, NS], F32, name="y_t%d" % j) for j in range(8)]
        vec_rows = keep.tile([P, P], BF16, name="vec_rows")
        nc.vector.memset(vec_rows[:], 0.0)

        def load_a(c):
            nc.sync.dma_start(
                out=a_raw[c][:], in_=A[K_PASS * c : K_PASS * (c + 1), :].rearrange("(p j) s -> p j s", j=PACK)
            )

        def load_h(c):
            nc.sync.dma_start(
                out=h_raw[c][:], in_=h_tgt[K_PASS * c : K_PASS * (c + 1), :].rearrange("(p j) d -> p j d", j=PACK)
            )

        def load_w(g):
            nc.sync.dma_start(
                out=w_raw[g][:], in_=Wb0[K_PASS * g : K_PASS * (g + 1), :].rearrange("(r p) o -> p r o", p=P)
            )

        def load_vecs():
            for v, vec in enumerate((bb0, bn_b_gamma, bn_b_beta, bn_b_mean, bn_b_var)):
                nc.sync.dma_start(
                    out=vec_rows[8 * v : 8 * v + 8, :], in_=vec.rearrange("(r c) -> r c", c=P)
                )

        load_a(0)
        load_a(1)
        load_h(0)
        load_h(1)
        load_vecs()
        load_w(0)
        load_w(1)

        warm_in = keep.tile([P, 1], F32, name="warm_in")
        nc.vector.memset(warm_in[:], 1.0)
        ones = keep.tile([P, 8], BF16, name="ones")
        nc.vector.memset(ones[:], 1.0)
        eps_bn = keep.tile([P, 1], F32, name="eps_bn")
        nc.vector.memset(eps_bn[:], EPS_BN)
        one = keep.tile([P, 1], F32, name="one")
        warm_out = keep.tile([P, 1], F32, name="warm_out")
        nc.scalar.sqrt(out=warm_out[:], in_=warm_in[:])
        ident_f = keep.tile([P, P], F32, name="ident_f")
        make_identity(nc, ident_f[:])
        ident_b = keep.tile([P, P], BF16, name="ident_b")
        nc.vector.tensor_copy(out=ident_b[:], in_=ident_f[:])

        vec_t = keep.tile([P, 40], F32, name="vec_t")
        std = keep.tile([P, 8], F32, name="std")
        rstd = keep.tile([P, 8], F32, name="rstd")
        sc = keep.tile([P, 8], F32, name="sc")
        diff = keep.tile([P, 8], F32, name="diff")
        prod = keep.tile([P, 8], F32, name="prod")
        sh = keep.tile([P, 8], F32, name="sh")
        vec_ps = {}

        def bn_transpose():
            vec_ps[0] = psum.tile([P, P], BF16, tag="bank", name="vec_ps")
            nc.tensor.transpose(vec_ps[0][:], vec_rows[:], ident_b[:])

        def bn_copy():
            nc.scalar.copy(out=vec_t[:], in_=vec_ps[0][:, 0:40])
            nc.scalar.activation(out=std[:], in_=vec_ps[0][:, 32:40], func=ACT.Sqrt, bias=eps_bn[:, 0:1])

        def bn_step(k):
            if k == 0:
                nc.vector.reciprocal(out=rstd[:], in_=std[:])
                nc.vector.tensor_tensor(out=diff[:], in0=vec_t[:, 0:8], in1=vec_t[:, 24:32], op=ALU.subtract)
            elif k == 1:
                nc.vector.tensor_tensor(out=sc[:], in0=vec_t[:, 8:16], in1=rstd[:], op=ALU.mult)
            elif k == 2:
                nc.vector.tensor_tensor(out=prod[:], in0=diff[:], in1=sc[:], op=ALU.mult)
            else:
                nc.vector.tensor_tensor(out=sh[:], in0=prod[:], in1=vec_t[:, 16:24], op=ALU.add)

        cs_ps = [psum.tile([P, 8], F32, tag="bank", name="cs_ps%d" % i) for i in range(4)]
        cs_cl = keep.tile([P, 4], F32, name="cs_cl")
        rec = keep.tile([P, 4], F32, name="rec")
        r_bc = {}

        def column_sums(c, i):
            for j in range(PACK):
                nc.tensor.matmul(
                    out=cs_ps[i][:],
                    lhsT=a_raw[c][:, j, P * i : P * (i + 1)],
                    rhs=ones[:],
                    start=(c == 0 and j == 0),
                    stop=(c == 1 and j == PACK - 1),
                )

        def reciprocals(hh):
            cols = slice(2 * hh, 2 * hh + 2)
            for i in range(2 * hh, 2 * hh + 2):
                nc.vector.tensor_scalar_max(out=cs_cl[:, i : i + 1], in0=cs_ps[i][:, 0:1], scalar1=EPS_ROW)
            nc.vector.reciprocal(out=rec[:, cols], in_=cs_cl[:, cols])

        def spread(hh):
            r_bc[hh] = psum.tile([P, HALF], F32, tag="bank", name="r_bc")
            for b in range(2):
                i = 2 * hh + b
                nc.tensor.transpose(
                    r_bc[hh][:, P * b : P * (b + 1)], rec[:, i : i + 1].to_broadcast([P, P]), ident_f[:]
                )

        def regroup(eng, dst, src):
            copies[eng](
                out=dst.rearrange("p (q i) j -> p q j i", i=4),
                in_=src.rearrange("p j (q i) -> p q j i", i=4),
            )

        def quantise(codes, scales, grouped):
            nc.vector.quantize_mx(out=codes.bitcast(FP8X4), scales=scales, in_=grouped)

        def regroup_h(c, g, lo, hi, eng):
            regroup(eng, h_grp[(c, g)][:, lo:hi, :], h_raw[c][:, :, 512 * g + lo : 512 * g + hi])

        def quantise_h(c, g):
            cols = slice(512 * g, 512 * (g + 1))
            quantise(h_codes[:, c, cols], h_scales[:, c, cols], h_grp[(c, g)][:].rearrange("p w j -> p (w j)"))

        def regroup_h_gpsimd(c, g, lo, hi):
            nc.gpsimd.tensor_scalar(
                out=h_grp[(c, g)][:, lo:hi, :],
                in0=h_raw[c][:, :, 512 * g + lo : 512 * g + hi].rearrange("p j w -> p w j"),
                scalar1=one[:, 0:1], scalar2=0.0, op0=ALU.mult, op1=ALU.add,
            )

        def regroup_w(g, f, lo, hi, eng):
            regroup(eng, w_grp[(g, f)][:, lo:hi, :], w_raw[g][:, :, 512 * f + lo : 512 * f + hi])

        def quantise_w(g, f, lo, hi):
            cols = slice(512 * f + lo, 512 * f + hi)
            quantise(w_codes[:, g, cols], w_scales[:, g, cols], w_grp[(g, f)][:, lo:hi, :].rearrange("p w j -> p (w j)"))

        def normalise_a(c, hh):
            nc.vector.tensor_tensor(
                out=a_grp[hh][:, c].rearrange("p (q i) j -> p q j i", i=4),
                in0=a_raw[c][:, :, HALF * hh : HALF * (hh + 1)].rearrange("p j (q i) -> p q j i", i=4),
                in1=r_bc[hh][:].rearrange("p (q i) -> p q i", i=4).unsqueeze(2).to_broadcast([P, HALF // 4, PACK, 4]),
                op=ALU.mult,
            )

        def quantise_a(hh):
            quantise(a_codes[hh][:], a_scales[hh][:], a_grp[hh][:].rearrange("p c s j -> p (c s j)"))

        agg_ps = {}

        def agg_block(hh, g, b):
            bank = psum.tile([P, PACK, P], F32, tag="bank", name="agg_ps")
            agg_ps[(hh, g, b)] = bank
            for t in range(PACK):
                d_cols = slice(K_PASS * g + P * t, K_PASS * g + P * (t + 1))
                for c in range(2):
                    s_cols = slice(HALF * c + P * b, HALF * c + P * (b + 1))
                    nc.tensor.matmul_mx(
                        out=bank[:, t, :],
                        lhsT=h_codes[:, c, d_cols].bitcast(FP8X4),
                        lhsT_scale=h_scales[:, c, d_cols],
                        rhs=a_codes[hh][:, s_cols].bitcast(FP8X4),
                        rhs_scale=a_scales[hh][:, s_cols],
                        start=(c == 0),
                        stop=(c == 1),
                    )

        def agg_out(hh, g, b, eng):
            s0 = HALF * hh + P * b
            copies[eng](out=g_grp[g][:, s0 : s0 + P, :], in_=agg_ps[(hh, g, b)][:].rearrange("p t s -> p s t"))

        def quantise_agg(hh, g):
            cols = slice(HALF * hh, HALF * (hh + 1))
            quantise(g_codes[:, g, cols], g_scales[:, g, cols], g_grp[g][:, cols, :].rearrange("p s t -> p (s t)"))

        h_ps = {}

        def layer(hh, j):
            if j % 2 == 0:
                h_ps[(hh, j // 2)] = psum.tile([P, 2, HALF], F32, tag="bank", name="h_ps")
            o_cols = slice(P * j, P * (j + 1))
            s_cols = slice(HALF * hh, HALF * (hh + 1))
            for g in range(2):
                nc.tensor.matmul_mx(
                    out=h_ps[(hh, j // 2)][:, j % 2, :],
                    lhsT=w_codes[:, g, o_cols].bitcast(FP8X4),
                    lhsT_scale=w_scales[:, g, o_cols],
                    rhs=g_codes[:, g, s_cols].bitcast(FP8X4),
                    rhs_scale=g_scales[:, g, s_cols],
                    start=(g == 0),
                    stop=(g == 1),
                )

        def scale_shift(hh, j, eng):
            y = y_t[j][:, HALF * hh : HALF * (hh + 1)]
            x = h_ps[(hh, j // 2)][:, j % 2, :]
            if eng == "s":
                nc.scalar.activation(out=y, in_=x, func=ACT.Identity, bias=sh[:, j : j + 1], scale=sc[:, j : j + 1])
            else:
                nc.vector.tensor_scalar(
                    out=y, in0=x, scalar1=sc[:, j : j + 1], scalar2=sh[:, j : j + 1], op0=ALU.mult, op1=ALU.add
                )

        o_ps = {}

        def turn_back(i, f):
            bank = psum.tile([P, 512], F32, tag="bank", name="o_ps")
            o_ps[(i, f)] = bank
            for jj in range(4):
                nc.tensor.transpose(
                    bank[:, P * jj : P * (jj + 1)], y_t[4 * f + jj][:, P * i : P * (i + 1)], ident_f[:]
                )

        def relu_store(i, f, eng):
            o_sb = keep.tile([P, 512], F32, name="o_sb%d%d" % (i, f))
            if eng == "s":
                nc.scalar.activation(out=o_sb[:], in_=o_ps[(i, f)][:], func=ACT.Relu)
            else:
                nc.vector.tensor_scalar_max(out=o_sb[:], in0=o_ps[(i, f)][:], scalar1=0.0)
            nc.sync.dma_start(out=out[P * i : P * (i + 1), 512 * f : 512 * (f + 1)], in_=o_sb[:])

        for c in range(2):
            for i in range(4):
                column_sums(c, i)
        reciprocals(0)
        reciprocals(1)
        spread(0)
        spread(1)
        bn_transpose()
        regroup_h(0, 0, 0, 512, "s")
        nc.vector.memset(one[:], 1.0)
        normalise_a(0, 0)
        normalise_a(1, 0)
        regroup_h_gpsimd(0, 1, 0, 512)
        regroup_h(1, 0, 0, 512, "s")
        normalise_a(0, 1)
        quantise_h(0, 0)
        quantise_a(0)
        regroup_h(1, 1, 0, 256, "v")
        regroup_h(1, 1, 256, 512, "s")
        bn_copy()
        quantise_h(1, 0)
        agg_block(0, 0, 0)
        agg_block(0, 0, 1)
        quantise_h(0, 1)
        normalise_a(1, 1)
        bn_step(0)
        regroup_w(0, 0, 0, 512, "s")
        quantise_h(1, 1)
        bn_step(1)
        agg_block(0, 1, 0)
        agg_block(0, 1, 1)
        quantise_a(1)
        bn_step(2)
        agg_block(1, 0, 0)
        agg_block(1, 0, 1)
        agg_block(1, 1, 0)
        agg_block(1, 1, 1)
        for g in range(2):
            for b in range(2):
                agg_out(0, g, b, "s")
        regroup_w(1, 0, 0, 512, "v")
        bn_step(3)
        quantise_w(0, 0, 0, 512)
        quantise_agg(0, 0)
        quantise_w(1, 0, 0, 512)
        quantise_agg(0, 1)
        agg_out(1, 0, 0, "s")
        agg_out(1, 0, 1, "s")
        for j in range(4):
            layer(0, j)
        agg_out(1, 1, 0, "s")
        agg_out(1, 1, 1, "s")
        regroup_w(0, 1, 0, 512, "v")
        quantise_agg(1, 0)
        quantise_agg(1, 1)
        regroup_w(1, 1, 0, 256, "v")
        for j in range(4):
            layer(1, j)
        for j in range(4):
            scale_shift(0, j, "s")
        quantise_w(0, 1, 0, 512)
        for i in range(2):
            turn_back(i, 0)
        regroup_w(1, 1, 256, 512, "v")
        for j in range(4):
            scale_shift(1, j, "s")
        quantise_w(1, 1, 0, 256)
        quantise_w(1, 1, 256, 512)
        for i in range(2, 4):
            turn_back(i, 0)
        for j in range(4, 8):
            layer(0, j)
        for j in range(4, 8):
            layer(1, j)
        relu_store(0, 0, "s")
        relu_store(1, 0, "v")
        relu_store(2, 0, "s")
        relu_store(3, 0, "v")
        for j in range(4, 8):
            scale_shift(0, j, "v" if j < 6 else "s")
        for i in range(2):
            turn_back(i, 1)
        for j in range(4, 8):
            scale_shift(1, j, "v" if j < 6 else "s")
        for i in range(2):
            relu_store(i, 1, "v" if i % 2 else "s")
        for i in range(2, 4):
            turn_back(i, 1)
        for i in range(2, 4):
            relu_store(i, 1, "v" if i % 2 else "s")
